import numpy as np
import ml_dtypes


def mxq(x, axis, fmt="e4m3"):
    dtype, down = {"e4m3": (ml_dtypes.float8_e4m3fn, 7), "e5m2": (ml_dtypes.float8_e5m2, 14)}[fmt]
    v = np.moveaxis(np.asarray(x, np.float32).astype(ml_dtypes.bfloat16).astype(np.float64), axis, -1)
    blocks = v.reshape(v.shape[:-1] + (-1, 32))
    amax = np.abs(blocks).max(-1, keepdims=True)
    byte = np.maximum(np.where(amax > 0, np.frexp(amax)[1] - 1 + 127, 0) - down, 1)
    scale = np.exp2(byte - 127.0)
    codes = (blocks / scale).astype(np.float32).astype(dtype).astype(np.float64)
    return np.moveaxis((codes * scale).reshape(v.shape), -1, axis)


WIDE = False


def mx_kscale(k):
    if not WIDE:
        return np.ones(k)
    levels = np.array([10, -10, 5, -5, 0])
    a = np.random.permutation(np.resize(levels, k // 512 * 4)).reshape(k // 512, 4)
    idx = np.arange(k)
    return np.exp2(a[idx // 512, idx % 128 // 32])


BF16 = ml_dtypes.bfloat16


def bf(x):
    return np.asarray(x, np.float32).astype(BF16)


def f64(x):
    return np.asarray(x).astype(np.float64)


E2M1 = np.array([0.0, 0.5, 1.0, 1.5, 2.0, 3.0, 4.0, 6.0, -0.0, -0.5, -1.0, -1.5, -2.0, -3.0, -4.0, -6.0])


def pack_weight(w, fmt):
    k, n = w.shape
    w = f64(bf(w)).reshape(k // 32, 32, n)
    amax = np.abs(w).max(1)
    if fmt == "e4m3":
        byte = np.frexp(amax)[1] - 1 + 127 - 7
    else:
        mant, ex = np.frexp(amax / 6.0)
        byte = np.where(mant > 0.5, ex, ex - 1) + 127
    byte = np.clip(np.where(amax > 0, byte, 1), 1, 254)
    scaled = (w * np.exp2(127.0 - byte)[:, None, :]).reshape(k, n).astype(np.float32)
    by_word = np.ascontiguousarray(scaled.reshape(k // 512, 128, 4, n).transpose(0, 1, 3, 2))
    if fmt == "e4m3":
        words = by_word.astype(ml_dtypes.float8_e4m3fn).view(np.uint8)
    else:
        c = by_word.astype(ml_dtypes.float4_e2m1fn).view(np.uint8) & 0xF
        words = c[..., 0::2] | (c[..., 1::2] << 4)
    return np.ascontiguousarray(words), np.ascontiguousarray(byte.astype(np.uint8).reshape(k // 512, 16, n))


def unpack_weight(words, scales, fmt):
    g, p, n, _ = words.shape
    if fmt == "e4m3":
        vals = np.ascontiguousarray(words).view(ml_dtypes.float8_e4m3fn).astype(np.float64)
    else:
        nib = np.empty((g, p, n, 4), np.uint8)
        nib[..., 0::2] = words & 0xF
        nib[..., 1::2] = words >> 4
        vals = E2M1[nib]
    vals = vals * np.repeat(np.exp2(scales.astype(np.float64) - 127.0), 8, axis=1)[..., None]
    return vals.transpose(0, 1, 3, 2).reshape(g * 512, n)

def pack4(w):
    words, scales = pack_weight(w, "e2m1")
    return words.reshape(words.shape[0], 128, -1), scales


def unpack4(words, scales):
    return unpack_weight(words.reshape(words.shape[0], 128, -1, 2), scales, "e2m1")


B, N, D = 24, 512, 256
C = 2 * D
EPS_BN = 1e-5
NEG_SLOPE = 0.01


def bn_lrelu(x, g, b):
    mean = np.mean(x, axis=(0, 2), keepdims=True)
    var = np.var(x, axis=(0, 2), keepdims=True)
    y = (x - mean) / np.sqrt(var + EPS_BN) * g[None, :, None] + b[None, :, None]
    return np.where(y >= 0, y, NEG_SLOPE * y)


def setup_inputs():
    s = mx_kscale(C)
    v = np.random.standard_normal((B, C, N))
    w2 = np.random.standard_normal((D, C)) / np.sqrt(C) / s[None, :]
    words, scales = pack4(np.ascontiguousarray(w2.T))
    return {"h1": bf(np.where(v >= 0, v, NEG_SLOPE * v) * s[None, :, None]),
            "W2_words": words,
            "W2_scales": scales,
            "g2": bf(1.0 + 0.2 * np.random.standard_normal(D)),
            "b2": bf(0.3 * np.random.standard_normal(D))}


def reference(h1, W2_words, W2_scales, g2, b2):
    z = unpack4(W2_words, W2_scales).T @ mxq(f64(h1), 1, "e4m3")
    return np.swapaxes(bn_lrelu(z, f64(g2), f64(b2)), 1, 2)

@@ -1,0 +1,226 @@
+from contextlib import ExitStack
+
+import concourse.mybir as mybir
+from concourse.masks import make_identity
+
+F32 = mybir.dt.float32
+BF16 = mybir.dt.bfloat16
+I32 = mybir.dt.int32
+U8 = mybir.dt.uint8
+U32 = mybir.dt.uint32
+FP8X4 = mybir.dt.float8_e4m3fn_x4
+FP4X4 = mybir.dt.float4_e2m1fn_x4
+ALU = mybir.AluOpType
+ACT = mybir.ActivationFunctionType
+AXIS = mybir.AxisListType
+
+P = 128
+PACK = 4
+GRAPHS = 24
+NODES = 512
+CH_IN = P * PACK
+CH_OUT = 256
+HALVES = CH_OUT // P
+COUNT = GRAPHS * NODES
+EPS_BN = 1e-5
+NEG_SLOPE = 0.01
+NODE_STEP = NODES // P
+
+FLOPS = 2 * GRAPHS * NODES * CH_IN * CH_OUT
+
+
+def tile_yuyipointupdate_pb_t_kernel(tc, h1, W2_words, W2_scales, g2, b2, out):
+    nc = tc.nc
+    with ExitStack() as pools:
+        const = pools.enter_context(tc.tile_pool(name="const", bufs=1))
+        raw_pool = pools.enter_context(tc.tile_pool(name="raw", bufs=6))
+        grouped_pool = pools.enter_context(tc.tile_pool(name="grouped", bufs=3))
+        work = pools.enter_context(tc.tile_pool(name="work", bufs=3))
+        psum_z = pools.enter_context(tc.psum_pool(name="psum_z", bufs=4))
+
+        one = const.tile([P, 1], F32)
+        nc.vector.memset(one[:], 1.0)
+        one_root = const.tile([P, 1], F32)
+        nc.scalar.activation(out=one_root[:], in_=one[:], func=ACT.Sqrt)
+
+        ident = const.tile([P, P], F32)
+        make_identity(nc, ident[:])
+
+        h_codes = const.tile([P, GRAPHS, NODES], U32, align_bytes=64)
+        h_scales = const.tile([P, GRAPHS, NODES], U8, align_bytes=64)
+
+        raw_tiles = {}
+
+        def load_graph(b):
+            raw = raw_pool.tile([P, PACK, NODES], BF16, name="raw")
+            nc.sync.dma_start(out=raw[:], in_=h1[b].rearrange("(p t) n -> p t n", t=PACK))
+            raw_tiles[b] = raw
+
+        load_graph(0)
+
+        w_words = const.tile([P, 2 * CH_OUT], U8, align_bytes=64)
+        nc.sync.dma_start(out=w_words[:].bitcast(I32), in_=W2_words[0].bitcast(I32))
+        w_scales = const.tile([P, CH_OUT], U8, align_bytes=64)
+        nc.vector.memset(w_scales[:].bitcast(I32), 0)
+        for quadrant in range(4):
+            nc.sync.dma_start(
+                out=w_scales[32 * quadrant : 32 * quadrant + 4, :].bitcast(I32),
+                in_=W2_scales[0, 4 * quadrant : 4 * quadrant + 4, :].bitcast(I32),
+            )
+
+        gb_rows = const.tile([P, P], BF16)
+        nc.vector.memset(gb_rows[:], 0.0)
+        nc.sync.dma_start(out=gb_rows[0:HALVES, :], in_=g2.rearrange("(h o) -> h o", h=HALVES))
+        nc.sync.dma_start(
+            out=gb_rows[HALVES : 2 * HALVES, :], in_=b2.rearrange("(h o) -> h o", h=HALVES)
+        )
+        gb_rows_f32 = const.tile([P, P], F32)
+        nc.vector.tensor_copy(out=gb_rows_f32[:], in_=gb_rows[:])
+        gain_shift = const.tile([P, 2 * HALVES], F32)
+
+        def multiply(acc, b, h, start, stop):
+            nc.tensor.matmul_mx(
+                out=acc,
+                lhsT=w_words[:, 2 * P * h : 2 * P * (h + 1)].bitcast(FP4X4),
+                lhsT_scale=w_scales[:, P * h : P * (h + 1)],
+                rhs=h_codes[:, b, :].bitcast(FP8X4),
+                rhs_scale=h_scales[:, b, :],
+                start=start,
+                stop=stop,
+            )
+
+        first_sum = const.tile([P, HALVES], F32)
+        neg_shift = const.tile([P, HALVES], F32)
+        square_sums = const.tile([P, HALVES, GRAPHS], F32)
+        z_total = const.tile([P, HALVES], F32)
+        grouped_tiles = {}
+
+        def regroup(b):
+            grouped = grouped_pool.tile([P, NODES, PACK], BF16, align_bytes=64, name="grouped")
+            nc.vector.tensor_copy(
+                out=grouped[:].rearrange("p (c i) t -> p c t i", i=4),
+                in_=raw_tiles[b][:].rearrange("p t (c i) -> p c t i", i=4),
+            )
+            grouped_tiles[b] = grouped
+
+        def quantise(b):
+            nc.vector.quantize_mx(
+                out=h_codes[:, b, :].bitcast(FP8X4),
+                scales=h_scales[:, b, :],
+                in_=grouped_tiles[b][:].rearrange("p n t -> p (n t)"),
+            )
+
+        with tc.psum_pool(name="psum_sum", bufs=1) as psum_sum:
+            gb_turned = psum_sum.tile([P, P], F32)
+            nc.tensor.transpose(out=gb_turned[:], in_=gb_rows_f32[:], identity=ident[:])
+            nc.vector.tensor_copy(out=gain_shift[:], in_=gb_turned[:, 0 : 2 * HALVES])
+
+            z_sums = [psum_sum.tile([P, NODES], F32, name="z_sum%d" % h) for h in range(HALVES)]
+
+            def statistics(b):
+                for h in range(HALVES):
+                    z = psum_z.tile([P, NODES], F32, name="z")
+                    multiply(z[:], b, h, True, True)
+                    multiply(z_sums[h][:], b, h, b == 0, b == GRAPHS - 1)
+                    squares = work.tile([P, NODES], F32, name="squares")
+                    if b == 0:
+                        nc.scalar.activation(
+                            out=squares[:], in_=z[:], func=ACT.Identity,
+                            accum_out=first_sum[:, h : h + 1],
+                        )
+                        nc.scalar.mul(
+                            out=neg_shift[:, h : h + 1], in_=first_sum[:, h : h + 1],
+                            mul=-1.0 / NODES,
+                        )
+                    nc.scalar.activation(
+                        out=squares[:], in_=z[:], func=ACT.Square,
+                        bias=neg_shift[:, h : h + 1],
+                        accum_out=square_sums[:, h, b : b + 1],
+                    )
+
+            regroup(0)
+            for b in range(1, GRAPHS):
+                load_graph(b)
+                regroup(b)
+                quantise(b - 1)
+                statistics(b - 1)
+            quantise(GRAPHS - 1)
+            statistics(GRAPHS - 1)
+
+            for h in range(HALVES):
+                nc.vector.tensor_reduce(
+                    out=z_total[:, h : h + 1], in_=z_sums[h][:], axis=AXIS.X, op=ALU.add
+                )
+
+        square_total = const.tile([P, HALVES], F32)
+        nc.vector.tensor_reduce(out=square_total[:], in_=square_sums[:], axis=AXIS.X, op=ALU.add)
+        mean = const.tile([P, HALVES], F32)
+        nc.vector.tensor_scalar(
+            out=mean[:], in0=z_total[:], scalar1=1.0 / COUNT, scalar2=None, op0=ALU.mult
+        )
+        offset = const.tile([P, HALVES], F32)
+        nc.vector.tensor_add(out=offset[:], in0=mean[:], in1=neg_shift[:])
+        offset_sq = const.tile([P, HALVES], F32)
+        nc.vector.tensor_mul(out=offset_sq[:], in0=offset[:], in1=offset[:])
+        var = const.tile([P, HALVES], F32)
+        nc.vector.scalar_tensor_tensor(
+            out=var[:], in0=square_total[:], scalar=1.0 / COUNT, in1=offset_sq[:],
+            op0=ALU.mult, op1=ALU.subtract,
+        )
+        var_eps = const.tile([P, HALVES], F32)
+        nc.vector.tensor_scalar(
+            out=var_eps[:], in0=var[:], scalar1=0.0, scalar2=EPS_BN, op0=ALU.max, op1=ALU.add
+        )
+        std = const.tile([P, HALVES], F32)
+        nc.scalar.activation(out=std[:], in_=var_eps[:], func=ACT.Sqrt)
+        inv_std = const.tile([P, HALVES], F32)
+        nc.vector.reciprocal(out=inv_std[:], in_=std[:])
+        scale = const.tile([P, HALVES], F32)
+        nc.vector.tensor_mul(out=scale[:], in0=gain_shift[:, 0:HALVES], in1=inv_std[:])
+        mean_scaled = const.tile([P, HALVES], F32)
+        nc.vector.tensor_mul(out=mean_scaled[:], in0=mean[:], in1=scale[:])
+        bias = const.tile([P, HALVES], F32)
+        nc.vector.tensor_sub(
+            out=bias[:], in0=gain_shift[:, HALVES : 2 * HALVES], in1=mean_scaled[:]
+        )
+
+        with tc.psum_pool(name="psum_t", bufs=4) as psum_t:
+            for b in range(GRAPHS):
+                y = work.tile([P, HALVES, NODES], F32, name="y")
+                for h in range(HALVES):
+                    z = psum_z.tile([P, NODES], F32, name="z")
+                    multiply(z[:], b, h, True, True)
+                    nc.scalar.activation(
+                        out=y[:, h, :].rearrange("p (j q) -> p j q", j=NODE_STEP),
+                        in_=z[:].rearrange("p (q j) -> p j q", j=NODE_STEP),
+                        func=ACT.Identity,
+                        scale=scale[:, h : h + 1],
+                        bias=bias[:, h : h + 1],
+                    )
+                r = work.tile([P, HALVES, NODES], F32, name="r")
+                nc.vector.scalar_tensor_tensor(
+                    out=r[:].rearrange("p h n -> p (h n)"),
+                    in0=y[:].rearrange("p h n -> p (h n)"),
+                    scalar=NEG_SLOPE,
+                    in1=y[:].rearrange("p h n -> p (h n)"),
+                    op0=ALU.mult,
+                    op1=ALU.max,
+                )
+                result = work.tile([P, NODE_STEP, CH_OUT], F32, name="result")
+                for pair in range(NODE_STEP // 2):
+                    turned = psum_t.tile([P, 2, CH_OUT], F32, name="turned")
+                    for i in range(2):
+                        j = 2 * pair + i
+                        for h in range(HALVES):
+                            nc.tensor.transpose(
+                                out=turned[:, i, P * h : P * (h + 1)],
+                                in_=r[:, h, P * j : P * (j + 1)],
+                                identity=ident[:],
+                            )
+                    if pair == 0:
+                        nc.scalar.copy(out=result[:, 0:2, :], in_=turned[:])
+                    else:
+                        nc.vector.tensor_copy(out=result[:, 2:4, :], in_=turned[:])
+                nc.sync.dma_start(
+                    out=out[b].rearrange("(q j) o -> q j o", j=NODE_STEP), in_=result[:]
+                )

@@ -29,13 +29,14 @@ NODE_STEP = NODES // P
 FLOPS = 2 * GRAPHS * NODES * CH_IN * CH_OUT
 
 
+SCALAR_EVERY = 6
+
+
 def tile_yuyipointupdate_pb_t_kernel(tc, h1, W2_words, W2_scales, g2, b2, out):
     nc = tc.nc
     with ExitStack() as pools:
+        pools.enter_context(tc.manual_schedule())
         const = pools.enter_context(tc.tile_pool(name="const", bufs=1))
-        raw_pool = pools.enter_context(tc.tile_pool(name="raw", bufs=6))
-        grouped_pool = pools.enter_context(tc.tile_pool(name="grouped", bufs=3))
-        work = pools.enter_context(tc.tile_pool(name="work", bufs=3))
         psum_z = pools.enter_context(tc.psum_pool(name="psum_z", bufs=4))
 
         one = const.tile([P, 1], F32)
@@ -43,40 +44,19 @@ def tile_yuyipointupdate_pb_t_kernel(tc, h1, W2_words, W2_scales, g2, b2, out):
         one_root = const.tile([P, 1], F32)
         nc.scalar.activation(out=one_root[:], in_=one[:], func=ACT.Sqrt)
 
+        ident_bf16 = const.tile([P, P], BF16)
+        make_identity(nc, ident_bf16[:])
         ident = const.tile([P, P], F32)
         make_identity(nc, ident[:])
 
         h_codes = const.tile([P, GRAPHS, NODES], U32, align_bytes=64)
         h_scales = const.tile([P, GRAPHS, NODES], U8, align_bytes=64)
-
-        raw_tiles = {}
-
-        def load_graph(b):
-            raw = raw_pool.tile([P, PACK, NODES], BF16, name="raw")
-            nc.sync.dma_start(out=raw[:], in_=h1[b].rearrange("(p t) n -> p t n", t=PACK))
-            raw_tiles[b] = raw
-
-        load_graph(0)
-
         w_words = const.tile([P, 2 * CH_OUT], U8, align_bytes=64)
-        nc.sync.dma_start(out=w_words[:].bitcast(I32), in_=W2_words[0].bitcast(I32))
         w_scales = const.tile([P, CH_OUT], U8, align_bytes=64)
-        nc.vector.memset(w_scales[:].bitcast(I32), 0)
-        for quadrant in range(4):
-            nc.sync.dma_start(
-                out=w_scales[32 * quadrant : 32 * quadrant + 4, :].bitcast(I32),
-                in_=W2_scales[0, 4 * quadrant : 4 * quadrant + 4, :].bitcast(I32),
-            )
-
         gb_rows = const.tile([P, P], BF16)
-        nc.vector.memset(gb_rows[:], 0.0)
-        nc.sync.dma_start(out=gb_rows[0:HALVES, :], in_=g2.rearrange("(h o) -> h o", h=HALVES))
-        nc.sync.dma_start(
-            out=gb_rows[HALVES : 2 * HALVES, :], in_=b2.rearrange("(h o) -> h o", h=HALVES)
-        )
-        gb_rows_f32 = const.tile([P, P], F32)
-        nc.vector.tensor_copy(out=gb_rows_f32[:], in_=gb_rows[:])
         gain_shift = const.tile([P, 2 * HALVES], F32)
+        nc.vector.memset(w_scales[:].bitcast(I32), 0)
+        nc.vector.memset(gb_rows[:], 0.0)
 
         def multiply(acc, b, h, start, stop):
             nc.tensor.matmul_mx(
@@ -93,27 +73,54 @@ def tile_yuyipointupdate_pb_t_kernel(tc, h1, W2_words, W2_scales, g2, b2, out):
         neg_shift = const.tile([P, HALVES], F32)
         square_sums = const.tile([P, HALVES, GRAPHS], F32)
         z_total = const.tile([P, HALVES], F32)
-        grouped_tiles = {}
 
-        def regroup(b):
-            grouped = grouped_pool.tile([P, NODES, PACK], BF16, align_bytes=64, name="grouped")
-            nc.vector.tensor_copy(
-                out=grouped[:].rearrange("p (c i) t -> p c t i", i=4),
-                in_=raw_tiles[b][:].rearrange("p t (c i) -> p c t i", i=4),
+        with ExitStack() as sweep1:
+            raw_pool = sweep1.enter_context(tc.tile_pool(name="raw", bufs=GRAPHS))
+            grouped_pool = sweep1.enter_context(tc.tile_pool(name="grouped", bufs=4))
+            junk_pool = sweep1.enter_context(tc.tile_pool(name="junk", bufs=2))
+            psum_sum = sweep1.enter_context(tc.psum_pool(name="psum_sum", bufs=1))
+            raw_tiles = {}
+            grouped_tiles = {}
+
+            def load_graph(b):
+                raw = raw_pool.tile([P, PACK, NODES], BF16, name="raw")
+                nc.sync.dma_start(out=raw[:], in_=h1[b].rearrange("(p t) n -> p t n", t=PACK))
+                raw_tiles[b] = raw
+
+            load_graph(0)
+            nc.sync.dma_start(out=w_words[:].bitcast(I32), in_=W2_words[0].bitcast(I32))
+            for quadrant in range(4):
+                nc.sync.dma_start(
+                    out=w_scales[32 * quadrant : 32 * quadrant + 4, :].bitcast(I32),
+                    in_=W2_scales[0, 4 * quadrant : 4 * quadrant + 4, :].bitcast(I32),
+                )
+            load_graph(1)
+            nc.sync.dma_start(out=gb_rows[0:HALVES, :], in_=g2.rearrange("(h o) -> h o", h=HALVES))
+            nc.sync.dma_start(
+                out=gb_rows[HALVES : 2 * HALVES, :], in_=b2.rearrange("(h o) -> h o", h=HALVES)
             )
-            grouped_tiles[b] = grouped
+            for b in range(2, GRAPHS):
+                load_graph(b)
 
-        def quantise(b):
-            nc.vector.quantize_mx(
-                out=h_codes[:, b, :].bitcast(FP8X4),
-                scales=h_scales[:, b, :],
-                in_=grouped_tiles[b][:].rearrange("p n t -> p (n t)"),
-            )
+            def on_scalar(b):
+                return b % SCALAR_EVERY == 1
 
-        with tc.psum_pool(name="psum_sum", bufs=1) as psum_sum:
-            gb_turned = psum_sum.tile([P, P], F32)
-            nc.tensor.transpose(out=gb_turned[:], in_=gb_rows_f32[:], identity=ident[:])
-            nc.vector.tensor_copy(out=gain_shift[:], in_=gb_turned[:, 0 : 2 * HALVES])
+            def regroup(b):
+                grouped = grouped_pool.tile([P, NODES, PACK], BF16, align_bytes=64, name="grouped")
+                dst = grouped[:].rearrange("p (c i) t -> p c t i", i=4)
+                src = raw_tiles[b][:].rearrange("p t (c i) -> p c t i", i=4)
+                if on_scalar(b):
+                    nc.scalar.copy(out=dst, in_=src)
+                else:
+                    nc.vector.tensor_copy(out=dst, in_=src)
+                grouped_tiles[b] = grouped
+
+            def quantise(b):
+                nc.vector.quantize_mx(
+                    out=h_codes[:, b, :].bitcast(FP8X4),
+                    scales=h_scales[:, b, :],
+                    in_=grouped_tiles[b][:].rearrange("p n t -> p (n t)"),
+                )
 
             z_sums = [psum_sum.tile([P, NODES], F32, name="z_sum%d" % h) for h in range(HALVES)]
 
@@ -122,7 +129,7 @@ def tile_yuyipointupdate_pb_t_kernel(tc, h1, W2_words, W2_scales, g2, b2, out):
                     z = psum_z.tile([P, NODES], F32, name="z")
                     multiply(z[:], b, h, True, True)
                     multiply(z_sums[h][:], b, h, b == 0, b == GRAPHS - 1)
-                    squares = work.tile([P, NODES], F32, name="squares")
+                    squares = junk_pool.tile([P, NODES], F32, name="squares")
                     if b == 0:
                         nc.scalar.activation(
                             out=squares[:], in_=z[:], func=ACT.Identity,
@@ -139,13 +146,17 @@ def tile_yuyipointupdate_pb_t_kernel(tc, h1, W2_words, W2_scales, g2, b2, out):
                     )
 
             regroup(0)
-            for b in range(1, GRAPHS):
-                load_graph(b)
-                regroup(b)
-                quantise(b - 1)
-                statistics(b - 1)
-            quantise(GRAPHS - 1)
-            statistics(GRAPHS - 1)
+            regroup(1)
+            gb_turned = psum_sum.tile([P, P], BF16)
+            nc.tensor.transpose(out=gb_turned[:], in_=gb_rows[:], identity=ident_bf16[:])
+            nc.scalar.copy(out=gain_shift[:], in_=gb_turned[:, 0 : 2 * HALVES])
+            for b in range(GRAPHS):
+                if b + 2 < GRAPHS and on_scalar(b + 2):
+                    regroup(b + 2)
+                if 1 <= b + 1 < GRAPHS and not on_scalar(b + 1):
+                    regroup(b + 1)
+                quantise(b)
+                statistics(b)
 
             for h in range(HALVES):
                 nc.vector.tensor_reduce(
@@ -154,12 +165,11 @@ def tile_yuyipointupdate_pb_t_kernel(tc, h1, W2_words, W2_scales, g2, b2, out):
 
         square_total = const.tile([P, HALVES], F32)
         nc.vector.tensor_reduce(out=square_total[:], in_=square_sums[:], axis=AXIS.X, op=ALU.add)
-        mean = const.tile([P, HALVES], F32)
-        nc.vector.tensor_scalar(
-            out=mean[:], in0=z_total[:], scalar1=1.0 / COUNT, scalar2=None, op0=ALU.mult
-        )
         offset = const.tile([P, HALVES], F32)
-        nc.vector.tensor_add(out=offset[:], in0=mean[:], in1=neg_shift[:])
+        nc.vector.scalar_tensor_tensor(
+            out=offset[:], in0=z_total[:], scalar=1.0 / COUNT, in1=neg_shift[:],
+            op0=ALU.mult, op1=ALU.add,
+        )
         offset_sq = const.tile([P, HALVES], F32)
         nc.vector.tensor_mul(out=offset_sq[:], in0=offset[:], in1=offset[:])
         var = const.tile([P, HALVES], F32)
@@ -173,40 +183,56 @@ def tile_yuyipointupdate_pb_t_kernel(tc, h1, W2_words, W2_scales, g2, b2, out):
         )
         std = const.tile([P, HALVES], F32)
         nc.scalar.activation(out=std[:], in_=var_eps[:], func=ACT.Sqrt)
+        neg_mean_gain = const.tile([P, HALVES], F32)
+        nc.vector.scalar_tensor_tensor(
+            out=neg_mean_gain[:], in0=z_total[:], scalar=-1.0 / COUNT, in1=gain_shift[:, 0:HALVES],
+            op0=ALU.mult, op1=ALU.mult,
+        )
         inv_std = const.tile([P, HALVES], F32)
         nc.vector.reciprocal(out=inv_std[:], in_=std[:])
         scale = const.tile([P, HALVES], F32)
         nc.vector.tensor_mul(out=scale[:], in0=gain_shift[:, 0:HALVES], in1=inv_std[:])
-        mean_scaled = const.tile([P, HALVES], F32)
-        nc.vector.tensor_mul(out=mean_scaled[:], in0=mean[:], in1=scale[:])
         bias = const.tile([P, HALVES], F32)
-        nc.vector.tensor_sub(
-            out=bias[:], in0=gain_shift[:, HALVES : 2 * HALVES], in1=mean_scaled[:]
-        )
+        nc.vector.tensor_mul(out=bias[:], in0=neg_mean_gain[:], in1=inv_std[:])
+        nc.vector.tensor_add(out=bias[:], in0=bias[:], in1=gain_shift[:, HALVES : 2 * HALVES])
 
-        with tc.psum_pool(name="psum_t", bufs=4) as psum_t:
-            for b in range(GRAPHS):
-                y = work.tile([P, HALVES, NODES], F32, name="y")
+        with ExitStack() as sweep2:
+            work = sweep2.enter_context(tc.tile_pool(name="work", bufs=3))
+            result_pool = sweep2.enter_context(tc.tile_pool(name="result", bufs=4))
+            psum_t = sweep2.enter_context(tc.psum_pool(name="psum_t", bufs=4))
+            z_tiles = {}
+            y_tiles = {}
+            r_tiles = {}
+            turned_tiles = {}
+
+            def multiply_again(b):
                 for h in range(HALVES):
                     z = psum_z.tile([P, NODES], F32, name="z")
                     multiply(z[:], b, h, True, True)
+                    z_tiles[b, h] = z
+
+            def normalise(b):
+                y = work.tile([P, HALVES, NODES], F32, name="y")
+                for h in range(HALVES):
                     nc.scalar.activation(
                         out=y[:, h, :].rearrange("p (j q) -> p j q", j=NODE_STEP),
-                        in_=z[:].rearrange("p (q j) -> p j q", j=NODE_STEP),
+                        in_=z_tiles[b, h][:].rearrange("p (q j) -> p j q", j=NODE_STEP),
                         func=ACT.Identity,
                         scale=scale[:, h : h + 1],
                         bias=bias[:, h : h + 1],
                     )
+                y_tiles[b] = y
+
+            def leaky_relu(b):
                 r = work.tile([P, HALVES, NODES], F32, name="r")
+                y_flat = y_tiles[b][:].rearrange("p h n -> p (h n)")
                 nc.vector.scalar_tensor_tensor(
-                    out=r[:].rearrange("p h n -> p (h n)"),
-                    in0=y[:].rearrange("p h n -> p (h n)"),
-                    scalar=NEG_SLOPE,
-                    in1=y[:].rearrange("p h n -> p (h n)"),
-                    op0=ALU.mult,
-                    op1=ALU.max,
+                    out=r[:].rearrange("p h n -> p (h n)"), in0=y_flat, scalar=NEG_SLOPE,
+                    in1=y_flat, op0=ALU.mult, op1=ALU.max,
                 )
-                result = work.tile([P, NODE_STEP, CH_OUT], F32, name="result")
+                r_tiles[b] = r
+
+            def turn(b):
                 for pair in range(NODE_STEP // 2):
                     turned = psum_t.tile([P, 2, CH_OUT], F32, name="turned")
                     for i in range(2):
@@ -214,13 +240,28 @@ def tile_yuyipointupdate_pb_t_kernel(tc, h1, W2_words, W2_scales, g2, b2, out):
                         for h in range(HALVES):
                             nc.tensor.transpose(
                                 out=turned[:, i, P * h : P * (h + 1)],
-                                in_=r[:, h, P * j : P * (j + 1)],
+                                in_=r_tiles[b][:, h, P * j : P * (j + 1)],
                                 identity=ident[:],
                             )
-                    if pair == 0:
-                        nc.scalar.copy(out=result[:, 0:2, :], in_=turned[:])
-                    else:
-                        nc.vector.tensor_copy(out=result[:, 2:4, :], in_=turned[:])
+                    turned_tiles[b, pair] = turned
+
+            def copy_out_and_store(b):
+                result = result_pool.tile([P, NODE_STEP, CH_OUT], F32, name="result")
+                nc.scalar.copy(out=result[:, 0:2, :], in_=turned_tiles[b, 0][:])
+                nc.vector.tensor_copy(out=result[:, 2:4, :], in_=turned_tiles[b, 1][:])
                 nc.sync.dma_start(
                     out=out[b].rearrange("(q j) o -> q j o", j=NODE_STEP), in_=result[:]
                 )
+
+            multiply_again(0)
+            for step in range(GRAPHS + 3):
+                if 0 <= step - 2 < GRAPHS:
+                    turn(step - 2)
+                if step + 1 < GRAPHS:
+                    multiply_again(step + 1)
+                if step < GRAPHS:
+                    normalise(step)
+                if 0 <= step - 1 < GRAPHS:
+                    leaky_relu(step - 1)
+                if 0 <= step - 3 < GRAPHS:
+                    copy_out_and_store(step - 3)

@@ -29,7 +29,8 @@ NODE_STEP = NODES // P
 FLOPS = 2 * GRAPHS * NODES * CH_IN * CH_OUT
 
 
-SCALAR_EVERY = 6
+SCALAR_EVERY = 8
+SCALAR_AHEAD = 4
 
 
 def tile_yuyipointupdate_pb_t_kernel(tc, h1, W2_words, W2_scales, g2, b2, out):
@@ -42,7 +43,9 @@ def tile_yuyipointupdate_pb_t_kernel(tc, h1, W2_words, W2_scales, g2, b2, out):
         one = const.tile([P, 1], F32)
         nc.vector.memset(one[:], 1.0)
         one_root = const.tile([P, 1], F32)
-        nc.scalar.activation(out=one_root[:], in_=one[:], func=ACT.Sqrt)
+        nc.scalar.activation(out=one_root[:], in_=one[:], func=ACT.Abs_reciprocal_sqrt)
+        eps = const.tile([P, 1], F32)
+        nc.vector.memset(eps[:], EPS_BN)
 
         ident_bf16 = const.tile([P, P], BF16)
         make_identity(nc, ident_bf16[:])
@@ -58,18 +61,19 @@ def tile_yuyipointupdate_pb_t_kernel(tc, h1, W2_words, W2_scales, g2, b2, out):
         nc.vector.memset(w_scales[:].bitcast(I32), 0)
         nc.vector.memset(gb_rows[:], 0.0)
 
-        def multiply(acc, b, h, start, stop):
+        def multiply(acc, b, h, nodes, start, stop):
             nc.tensor.matmul_mx(
                 out=acc,
                 lhsT=w_words[:, 2 * P * h : 2 * P * (h + 1)].bitcast(FP4X4),
                 lhsT_scale=w_scales[:, P * h : P * (h + 1)],
-                rhs=h_codes[:, b, :].bitcast(FP8X4),
-                rhs_scale=h_scales[:, b, :],
+                rhs=h_codes[:, b, nodes].bitcast(FP8X4),
+                rhs_scale=h_scales[:, b, nodes],
                 start=start,
                 stop=stop,
             )
 
-        first_sum = const.tile([P, HALVES], F32)
+        all_nodes = slice(0, NODES)
+
         neg_shift = const.tile([P, HALVES], F32)
         square_sums = const.tile([P, HALVES, GRAPHS], F32)
         z_total = const.tile([P, HALVES], F32)
@@ -122,23 +126,21 @@ def tile_yuyipointupdate_pb_t_kernel(tc, h1, W2_words, W2_scales, g2, b2, out):
                     in_=grouped_tiles[b][:].rearrange("p n t -> p (n t)"),
                 )
 
-            z_sums = [psum_sum.tile([P, NODES], F32, name="z_sum%d" % h) for h in range(HALVES)]
+            z_sums = [psum_sum.tile([P, P], F32, name="z_sum%d" % h) for h in range(HALVES)]
 
             def statistics(b):
                 for h in range(HALVES):
                     z = psum_z.tile([P, NODES], F32, name="z")
-                    multiply(z[:], b, h, True, True)
-                    multiply(z_sums[h][:], b, h, b == 0, b == GRAPHS - 1)
+                    multiply(z[:], b, h, all_nodes, True, True)
+                    for block in range(NODE_STEP):
+                        multiply(
+                            z_sums[h][:], b, h, slice(P * block, P * (block + 1)),
+                            b == 0 and block == 0,
+                            b == GRAPHS - 1 and block == NODE_STEP - 1,
+                        )
                     squares = junk_pool.tile([P, NODES], F32, name="squares")
                     if b == 0:
-                        nc.scalar.activation(
-                            out=squares[:], in_=z[:], func=ACT.Identity,
-                            accum_out=first_sum[:, h : h + 1],
-                        )
-                        nc.scalar.mul(
-                            out=neg_shift[:, h : h + 1], in_=first_sum[:, h : h + 1],
-                            mul=-1.0 / NODES,
-                        )
+                        nc.scalar.mul(out=neg_shift[:, h : h + 1], in_=z[:, 0:1], mul=-1.0)
                     nc.scalar.activation(
                         out=squares[:], in_=z[:], func=ACT.Square,
                         bias=neg_shift[:, h : h + 1],
@@ -151,8 +153,8 @@ def tile_yuyipointupdate_pb_t_kernel(tc, h1, W2_words, W2_scales, g2, b2, out):
             nc.tensor.transpose(out=gb_turned[:], in_=gb_rows[:], identity=ident_bf16[:])
             nc.scalar.copy(out=gain_shift[:], in_=gb_turned[:, 0 : 2 * HALVES])
             for b in range(GRAPHS):
-                if b + 2 < GRAPHS and on_scalar(b + 2):
-                    regroup(b + 2)
+                if b + SCALAR_AHEAD < GRAPHS and on_scalar(b + SCALAR_AHEAD):
+                    regroup(b + SCALAR_AHEAD)
                 if 1 <= b + 1 < GRAPHS and not on_scalar(b + 1):
                     regroup(b + 1)
                 quantise(b)
@@ -163,33 +165,32 @@ def tile_yuyipointupdate_pb_t_kernel(tc, h1, W2_words, W2_scales, g2, b2, out):
                     out=z_total[:, h : h + 1], in_=z_sums[h][:], axis=AXIS.X, op=ALU.add
                 )
 
-        square_total = const.tile([P, HALVES], F32)
-        nc.vector.tensor_reduce(out=square_total[:], in_=square_sums[:], axis=AXIS.X, op=ALU.add)
         offset = const.tile([P, HALVES], F32)
         nc.vector.scalar_tensor_tensor(
             out=offset[:], in0=z_total[:], scalar=1.0 / COUNT, in1=neg_shift[:],
             op0=ALU.mult, op1=ALU.add,
         )
-        offset_sq = const.tile([P, HALVES], F32)
-        nc.vector.tensor_mul(out=offset_sq[:], in0=offset[:], in1=offset[:])
+        neg_offset_sq = const.tile([P, HALVES], F32)
+        nc.vector.scalar_tensor_tensor(
+            out=neg_offset_sq[:], in0=offset[:], scalar=-1.0, in1=offset[:],
+            op0=ALU.mult, op1=ALU.mult,
+        )
+        square_total = const.tile([P, HALVES], F32)
+        nc.vector.tensor_reduce(out=square_total[:], in_=square_sums[:], axis=AXIS.X, op=ALU.add)
         var = const.tile([P, HALVES], F32)
         nc.vector.scalar_tensor_tensor(
-            out=var[:], in0=square_total[:], scalar=1.0 / COUNT, in1=offset_sq[:],
-            op0=ALU.mult, op1=ALU.subtract,
+            out=var[:], in0=square_total[:], scalar=1.0 / COUNT, in1=neg_offset_sq[:],
+            op0=ALU.mult, op1=ALU.add,
         )
-        var_eps = const.tile([P, HALVES], F32)
-        nc.vector.tensor_scalar(
-            out=var_eps[:], in0=var[:], scalar1=0.0, scalar2=EPS_BN, op0=ALU.max, op1=ALU.add
+        inv_std = const.tile([P, HALVES], F32)
+        nc.scalar.activation(
+            out=inv_std[:], in_=var[:], func=ACT.Abs_reciprocal_sqrt, bias=eps[:]
         )
-        std = const.tile([P, HALVES], F32)
-        nc.scalar.activation(out=std[:], in_=var_eps[:], func=ACT.Sqrt)
         neg_mean_gain = const.tile([P, HALVES], F32)
         nc.vector.scalar_tensor_tensor(
             out=neg_mean_gain[:], in0=z_total[:], scalar=-1.0 / COUNT, in1=gain_shift[:, 0:HALVES],
             op0=ALU.mult, op1=ALU.mult,
         )
-        inv_std = const.tile([P, HALVES], F32)
-        nc.vector.reciprocal(out=inv_std[:], in_=std[:])
         scale = const.tile([P, HALVES], F32)
         nc.vector.tensor_mul(out=scale[:], in0=gain_shift[:, 0:HALVES], in1=inv_std[:])
         bias = const.tile([P, HALVES], F32)
@@ -198,7 +199,7 @@ def tile_yuyipointupdate_pb_t_kernel(tc, h1, W2_words, W2_scales, g2, b2, out):
 
         with ExitStack() as sweep2:
             work = sweep2.enter_context(tc.tile_pool(name="work", bufs=3))
-            result_pool = sweep2.enter_context(tc.tile_pool(name="result", bufs=4))
+            result_pool = sweep2.enter_context(tc.tile_pool(name="result", bufs=8))
             psum_t = sweep2.enter_context(tc.psum_pool(name="psum_t", bufs=4))
             z_tiles = {}
             y_tiles = {}
@@ -208,7 +209,7 @@ def tile_yuyipointupdate_pb_t_kernel(tc, h1, W2_words, W2_scales, g2, b2, out):
             def multiply_again(b):
                 for h in range(HALVES):
                     z = psum_z.tile([P, NODES], F32, name="z")
-                    multiply(z[:], b, h, True, True)
+                    multiply(z[:], b, h, all_nodes, True, True)
                     z_tiles[b, h] = z
 
             def normalise(b):
@@ -246,12 +247,14 @@ def tile_yuyipointupdate_pb_t_kernel(tc, h1, W2_words, W2_scales, g2, b2, out):
                     turned_tiles[b, pair] = turned
 
             def copy_out_and_store(b):
-                result = result_pool.tile([P, NODE_STEP, CH_OUT], F32, name="result")
-                nc.scalar.copy(out=result[:, 0:2, :], in_=turned_tiles[b, 0][:])
-                nc.vector.tensor_copy(out=result[:, 2:4, :], in_=turned_tiles[b, 1][:])
-                nc.sync.dma_start(
-                    out=out[b].rearrange("(q j) o -> q j o", j=NODE_STEP), in_=result[:]
-                )
+                rows = out[b].rearrange("(q j) o -> q j o", j=NODE_STEP)
+                for pair in range(NODE_STEP // 2):
+                    result = result_pool.tile([P, 2, CH_OUT], F32, name="result")
+                    if pair == 0:
+                        nc.scalar.copy(out=result[:], in_=turned_tiles[b, pair][:])
+                    else:
+                        nc.vector.tensor_copy(out=result[:], in_=turned_tiles[b, pair][:])
+                    nc.sync.dma_start(out=rows[:, 2 * pair : 2 * pair + 2, :], in_=result[:])
 
             multiply_again(0)
             for step in range(GRAPHS + 3):

@@ -29,7 +29,7 @@ NODE_STEP = NODES // P
 FLOPS = 2 * GRAPHS * NODES * CH_IN * CH_OUT
 
 
-SCALAR_EVERY = 8
+SCALAR_EVERY = 6
 SCALAR_AHEAD = 4
 
 

@@ -91,19 +91,21 @@ def tile_yuyipointupdate_pb_t_kernel(tc, h1, W2_words, W2_scales, g2, b2, out):
                 nc.sync.dma_start(out=raw[:], in_=h1[b].rearrange("(p t) n -> p t n", t=PACK))
                 raw_tiles[b] = raw
 
-            load_graph(0)
+            for b in range(3):
+                load_graph(b)
             nc.sync.dma_start(out=w_words[:].bitcast(I32), in_=W2_words[0].bitcast(I32))
             for quadrant in range(4):
                 nc.sync.dma_start(
                     out=w_scales[32 * quadrant : 32 * quadrant + 4, :].bitcast(I32),
                     in_=W2_scales[0, 4 * quadrant : 4 * quadrant + 4, :].bitcast(I32),
                 )
-            load_graph(1)
+            for b in range(3, 6):
+                load_graph(b)
             nc.sync.dma_start(out=gb_rows[0:HALVES, :], in_=g2.rearrange("(h o) -> h o", h=HALVES))
             nc.sync.dma_start(
                 out=gb_rows[HALVES : 2 * HALVES, :], in_=b2.rearrange("(h o) -> h o", h=HALVES)
             )
-            for b in range(2, GRAPHS):
+            for b in range(6, GRAPHS):
                 load_graph(b)
 
             def on_scalar(b):
@@ -149,9 +151,6 @@ def tile_yuyipointupdate_pb_t_kernel(tc, h1, W2_words, W2_scales, g2, b2, out):
 
             regroup(0)
             regroup(1)
-            gb_turned = psum_sum.tile([P, P], BF16)
-            nc.tensor.transpose(out=gb_turned[:], in_=gb_rows[:], identity=ident_bf16[:])
-            nc.scalar.copy(out=gain_shift[:], in_=gb_turned[:, 0 : 2 * HALVES])
             for b in range(GRAPHS):
                 if b + SCALAR_AHEAD < GRAPHS and on_scalar(b + SCALAR_AHEAD):
                     regroup(b + SCALAR_AHEAD)
@@ -159,6 +158,10 @@ def tile_yuyipointupdate_pb_t_kernel(tc, h1, W2_words, W2_scales, g2, b2, out):
                     regroup(b + 1)
                 quantise(b)
                 statistics(b)
+                if b == 6:
+                    gb_turned = psum_sum.tile([P, P], BF16)
+                    nc.tensor.transpose(out=gb_turned[:], in_=gb_rows[:], identity=ident_bf16[:])
+                    nc.scalar.copy(out=gain_shift[:], in_=gb_turned[:, 0 : 2 * HALVES])
 
             for h in range(HALVES):
                 nc.vector.tensor_reduce(

@@ -99,14 +99,14 @@ def tile_yuyipointupdate_pb_t_kernel(tc, h1, W2_words, W2_scales, g2, b2, out):
                     out=w_scales[32 * quadrant : 32 * quadrant + 4, :].bitcast(I32),
                     in_=W2_scales[0, 4 * quadrant : 4 * quadrant + 4, :].bitcast(I32),
                 )
-            for b in range(3, 6):
+            for b in (3, 7, 4, 5, 6):
+                load_graph(b)
+            for b in range(8, GRAPHS):
                 load_graph(b)
             nc.sync.dma_start(out=gb_rows[0:HALVES, :], in_=g2.rearrange("(h o) -> h o", h=HALVES))
             nc.sync.dma_start(
                 out=gb_rows[HALVES : 2 * HALVES, :], in_=b2.rearrange("(h o) -> h o", h=HALVES)
             )
-            for b in range(6, GRAPHS):
-                load_graph(b)
 
             def on_scalar(b):
                 return b % SCALAR_EVERY == 1
@@ -158,7 +158,7 @@ def tile_yuyipointupdate_pb_t_kernel(tc, h1, W2_words, W2_scales, g2, b2, out):
                     regroup(b + 1)
                 quantise(b)
                 statistics(b)
-                if b == 6:
+                if b == GRAPHS - 3:
                     gb_turned = psum_sum.tile([P, P], BF16)
                     nc.tensor.transpose(out=gb_turned[:], in_=gb_rows[:], identity=ident_bf16[:])
                     nc.scalar.copy(out=gain_shift[:], in_=gb_turned[:, 0 : 2 * HALVES])

@@ -44,8 +44,6 @@ def tile_yuyipointupdate_pb_t_kernel(tc, h1, W2_words, W2_scales, g2, b2, out):
         nc.vector.memset(one[:], 1.0)
         one_root = const.tile([P, 1], F32)
         nc.scalar.activation(out=one_root[:], in_=one[:], func=ACT.Abs_reciprocal_sqrt)
-        eps = const.tile([P, 1], F32)
-        nc.vector.memset(eps[:], EPS_BN)
 
         ident_bf16 = const.tile([P, P], BF16)
         make_identity(nc, ident_bf16[:])
@@ -75,8 +73,10 @@ def tile_yuyipointupdate_pb_t_kernel(tc, h1, W2_words, W2_scales, g2, b2, out):
         all_nodes = slice(0, NODES)
 
         neg_shift = const.tile([P, HALVES], F32)
-        square_sums = const.tile([P, HALVES, GRAPHS], F32)
+        square_sums = const.tile([P, HALVES, GRAPHS - 1], F32)
+        square_last = const.tile([P, HALVES], F32)
         z_total = const.tile([P, HALVES], F32)
+        square_part = const.tile([P, HALVES], F32)
 
         with ExitStack() as sweep1:
             raw_pool = sweep1.enter_context(tc.tile_pool(name="raw", bufs=GRAPHS))
@@ -146,7 +146,9 @@ def tile_yuyipointupdate_pb_t_kernel(tc, h1, W2_words, W2_scales, g2, b2, out):
                     nc.scalar.activation(
                         out=squares[:], in_=z[:], func=ACT.Square,
                         bias=neg_shift[:, h : h + 1],
-                        accum_out=square_sums[:, h, b : b + 1],
+                        accum_out=(
+                            square_sums[:, h, b : b + 1] if b < GRAPHS - 1 else square_last[:, h : h + 1]
+                        ),
                     )
 
             regroup(0)
@@ -163,6 +165,13 @@ def tile_yuyipointupdate_pb_t_kernel(tc, h1, W2_words, W2_scales, g2, b2, out):
                     nc.tensor.transpose(out=gb_turned[:], in_=gb_rows[:], identity=ident_bf16[:])
                     nc.scalar.copy(out=gain_shift[:], in_=gb_turned[:, 0 : 2 * HALVES])
 
+            nc.vector.tensor_reduce(
+                out=square_part[:], in_=square_sums[:], axis=AXIS.X, op=ALU.add
+            )
+            nc.vector.tensor_scalar(
+                out=square_part[:], in0=square_part[:], scalar1=1.0 / COUNT, scalar2=EPS_BN,
+                op0=ALU.mult, op1=ALU.add,
+            )
             for h in range(HALVES):
                 nc.vector.tensor_reduce(
                     out=z_total[:, h : h + 1], in_=z_sums[h][:], axis=AXIS.X, op=ALU.add
@@ -173,32 +182,35 @@ def tile_yuyipointupdate_pb_t_kernel(tc, h1, W2_words, W2_scales, g2, b2, out):
             out=offset[:], in0=z_total[:], scalar=1.0 / COUNT, in1=neg_shift[:],
             op0=ALU.mult, op1=ALU.add,
         )
-        neg_offset_sq = const.tile([P, HALVES], F32)
-        nc.vector.scalar_tensor_tensor(
-            out=neg_offset_sq[:], in0=offset[:], scalar=-1.0, in1=offset[:],
-            op0=ALU.mult, op1=ALU.mult,
-        )
-        square_total = const.tile([P, HALVES], F32)
-        nc.vector.tensor_reduce(out=square_total[:], in_=square_sums[:], axis=AXIS.X, op=ALU.add)
-        var = const.tile([P, HALVES], F32)
-        nc.vector.scalar_tensor_tensor(
-            out=var[:], in0=square_total[:], scalar=1.0 / COUNT, in1=neg_offset_sq[:],
-            op0=ALU.mult, op1=ALU.add,
-        )
-        inv_std = const.tile([P, HALVES], F32)
-        nc.scalar.activation(
-            out=inv_std[:], in_=var[:], func=ACT.Abs_reciprocal_sqrt, bias=eps[:]
-        )
         neg_mean_gain = const.tile([P, HALVES], F32)
         nc.vector.scalar_tensor_tensor(
             out=neg_mean_gain[:], in0=z_total[:], scalar=-1.0 / COUNT, in1=gain_shift[:, 0:HALVES],
             op0=ALU.mult, op1=ALU.mult,
         )
-        scale = const.tile([P, HALVES], F32)
-        nc.vector.tensor_mul(out=scale[:], in0=gain_shift[:, 0:HALVES], in1=inv_std[:])
-        bias = const.tile([P, HALVES], F32)
-        nc.vector.tensor_mul(out=bias[:], in0=neg_mean_gain[:], in1=inv_std[:])
-        nc.vector.tensor_add(out=bias[:], in0=bias[:], in1=gain_shift[:, HALVES : 2 * HALVES])
+        offset_sq = const.tile([P, HALVES], F32)
+        nc.vector.tensor_mul(out=offset_sq[:], in0=offset[:], in1=offset[:])
+        rest = const.tile([P, HALVES], F32)
+        nc.vector.tensor_sub(out=rest[:], in0=square_part[:], in1=offset_sq[:])
+        inv_std = [const.tile([P, 1], F32, name="inv_std%d" % h) for h in range(HALVES)]
+        scale = [const.tile([P, 1], F32, name="scale%d" % h) for h in range(HALVES)]
+        bias = [const.tile([P, 1], F32, name="bias%d" % h) for h in range(HALVES)]
+        for h in (1, 0):
+            nc.scalar.activation(
+                out=inv_std[h][:], in_=square_last[:, h : h + 1],
+                func=ACT.Abs_reciprocal_sqrt, scale=1.0 / COUNT, bias=rest[:, h : h + 1],
+            )
+        nc.scalar.activation(
+            out=scale[0][:], in_=inv_std[0][:], func=ACT.Copy, scale=gain_shift[:, 0:1]
+        )
+        nc.scalar.activation(
+            out=bias[0][:], in_=inv_std[0][:], func=ACT.Identity,
+            scale=neg_mean_gain[:, 0:1], bias=gain_shift[:, HALVES : HALVES + 1],
+        )
+        nc.vector.tensor_mul(out=scale[1][:], in0=gain_shift[:, 1:2], in1=inv_std[1][:])
+        nc.vector.scalar_tensor_tensor(
+            out=bias[1][:], in0=inv_std[1][:], scalar=neg_mean_gain[:, 1:2],
+            in1=gain_shift[:, HALVES + 1 : HALVES + 2], op0=ALU.mult, op1=ALU.add,
+        )
 
         with ExitStack() as sweep2:
             work = sweep2.enter_context(tc.tile_pool(name="work", bufs=3))
@@ -206,35 +218,29 @@ def tile_yuyipointupdate_pb_t_kernel(tc, h1, W2_words, W2_scales, g2, b2, out):
             psum_t = sweep2.enter_context(tc.psum_pool(name="psum_t", bufs=4))
             z_tiles = {}
             y_tiles = {}
-            r_tiles = {}
             turned_tiles = {}
+            small_tiles = {}
 
             def multiply_again(b):
                 for h in range(HALVES):
                     z = psum_z.tile([P, NODES], F32, name="z")
                     multiply(z[:], b, h, all_nodes, True, True)
                     z_tiles[b, h] = z
+                y_tiles[b] = work.tile([P, HALVES, NODES], F32, name="y")
 
-            def normalise(b):
-                y = work.tile([P, HALVES, NODES], F32, name="y")
-                for h in range(HALVES):
+            def normalise(b, h, engine):
+                y = y_tiles[b][:, h, :].rearrange("p (j q) -> p j q", j=NODE_STEP)
+                z = z_tiles[b, h][:].rearrange("p (q j) -> p j q", j=NODE_STEP)
+                if engine == "scalar":
                     nc.scalar.activation(
-                        out=y[:, h, :].rearrange("p (j q) -> p j q", j=NODE_STEP),
-                        in_=z_tiles[b, h][:].rearrange("p (q j) -> p j q", j=NODE_STEP),
-                        func=ACT.Identity,
-                        scale=scale[:, h : h + 1],
-                        bias=bias[:, h : h + 1],
+                        out=y, in_=z, func=ACT.Identity,
+                        scale=scale[h][:], bias=bias[h][:],
                     )
-                y_tiles[b] = y
-
-            def leaky_relu(b):
-                r = work.tile([P, HALVES, NODES], F32, name="r")
-                y_flat = y_tiles[b][:].rearrange("p h n -> p (h n)")
-                nc.vector.scalar_tensor_tensor(
-                    out=r[:].rearrange("p h n -> p (h n)"), in0=y_flat, scalar=NEG_SLOPE,
-                    in1=y_flat, op0=ALU.mult, op1=ALU.max,
-                )
-                r_tiles[b] = r
+                else:
+                    nc.vector.tensor_scalar(
+                        out=y, in0=z, scalar1=scale[h][:], scalar2=bias[h][:],
+                        op0=ALU.mult, op1=ALU.add,
+                    )
 
             def turn(b):
                 for pair in range(NODE_STEP // 2):
@@ -244,30 +250,36 @@ def tile_yuyipointupdate_pb_t_kernel(tc, h1, W2_words, W2_scales, g2, b2, out):
                         for h in range(HALVES):
                             nc.tensor.transpose(
                                 out=turned[:, i, P * h : P * (h + 1)],
-                                in_=r_tiles[b][:, h, P * j : P * (j + 1)],
+                                in_=y_tiles[b][:, h, P * j : P * (j + 1)],
                                 identity=ident[:],
                             )
                     turned_tiles[b, pair] = turned
 
-            def copy_out_and_store(b):
+            def shrink(b, pair):
+                small = work.tile([P, 2, CH_OUT], F32, name="small")
+                nc.scalar.mul(out=small[:], in_=turned_tiles[b, pair][:], mul=NEG_SLOPE)
+                small_tiles[b, pair] = small
+
+            def leaky_relu_and_store(b, pair):
                 rows = out[b].rearrange("(q j) o -> q j o", j=NODE_STEP)
-                for pair in range(NODE_STEP // 2):
-                    result = result_pool.tile([P, 2, CH_OUT], F32, name="result")
-                    if pair == 0:
-                        nc.scalar.copy(out=result[:], in_=turned_tiles[b, pair][:])
-                    else:
-                        nc.vector.tensor_copy(out=result[:], in_=turned_tiles[b, pair][:])
-                    nc.sync.dma_start(out=rows[:, 2 * pair : 2 * pair + 2, :], in_=result[:])
+                result = result_pool.tile([P, 2, CH_OUT], F32, name="result")
+                nc.vector.tensor_max(
+                    out=result[:], in0=turned_tiles[b, pair][:], in1=small_tiles[b, pair][:]
+                )
+                nc.sync.dma_start(out=rows[:, 2 * pair : 2 * pair + 2, :], in_=result[:])
 
             multiply_again(0)
-            for step in range(GRAPHS + 3):
-                if 0 <= step - 2 < GRAPHS:
-                    turn(step - 2)
-                if step + 1 < GRAPHS:
-                    multiply_again(step + 1)
-                if step < GRAPHS:
-                    normalise(step)
+            multiply_again(1)
+            for step in range(GRAPHS + 2):
                 if 0 <= step - 1 < GRAPHS:
-                    leaky_relu(step - 1)
-                if 0 <= step - 3 < GRAPHS:
-                    copy_out_and_store(step - 3)
+                    turn(step - 1)
+                if step < GRAPHS:
+                    normalise(step, 0, "scalar")
+                    normalise(step, 1, "vector")
+                if step + 2 < GRAPHS:
+                    multiply_again(step + 2)
+                if 0 <= step - 2:
+                    for pair in range(NODE_STEP // 2):
+                        shrink(step - 2, pair)
+                    for pair in range(NODE_STEP // 2):
+                        leaky_relu_and_store(step - 2, pair)

@@ -130,16 +130,24 @@ def tile_yuyipointupdate_pb_t_kernel(tc, h1, W2_words, W2_scales, g2, b2, out):
 
             z_sums = [psum_sum.tile([P, P], F32, name="z_sum%d" % h) for h in range(HALVES)]
 
+            def add_to_sums(b, h):
+                for block in range(NODE_STEP):
+                    multiply(
+                        z_sums[h][:], b, h, slice(P * block, P * (block + 1)),
+                        b == 0 and block == 0,
+                        b == GRAPHS - 1 and block == NODE_STEP - 1,
+                    )
+
             def statistics(b):
+                last = b == GRAPHS - 1
+                if last:
+                    for h in range(HALVES):
+                        add_to_sums(b, h)
                 for h in range(HALVES):
                     z = psum_z.tile([P, NODES], F32, name="z")
                     multiply(z[:], b, h, all_nodes, True, True)
-                    for block in range(NODE_STEP):
-                        multiply(
-                            z_sums[h][:], b, h, slice(P * block, P * (block + 1)),
-                            b == 0 and block == 0,
-                            b == GRAPHS - 1 and block == NODE_STEP - 1,
-                        )
+                    if not last:
+                        add_to_sums(b, h)
                     squares = junk_pool.tile([P, NODES], F32, name="squares")
                     if b == 0:
                         nc.scalar.mul(out=neg_shift[:, h : h + 1], in_=z[:, 0:1], mul=-1.0)
@@ -165,6 +173,12 @@ def tile_yuyipointupdate_pb_t_kernel(tc, h1, W2_words, W2_scales, g2, b2, out):
                     nc.tensor.transpose(out=gb_turned[:], in_=gb_rows[:], identity=ident_bf16[:])
                     nc.scalar.copy(out=gain_shift[:], in_=gb_turned[:, 0 : 2 * HALVES])
 
+            def reduce_z(h):
+                nc.vector.tensor_reduce(
+                    out=z_total[:, h : h + 1], in_=z_sums[h][:], axis=AXIS.X, op=ALU.add
+                )
+
+            reduce_z(0)
             nc.vector.tensor_reduce(
                 out=square_part[:], in_=square_sums[:], axis=AXIS.X, op=ALU.add
             )
@@ -172,25 +186,22 @@ def tile_yuyipointupdate_pb_t_kernel(tc, h1, W2_words, W2_scales, g2, b2, out):
                 out=square_part[:], in0=square_part[:], scalar1=1.0 / COUNT, scalar2=EPS_BN,
                 op0=ALU.mult, op1=ALU.add,
             )
-            for h in range(HALVES):
-                nc.vector.tensor_reduce(
-                    out=z_total[:, h : h + 1], in_=z_sums[h][:], axis=AXIS.X, op=ALU.add
-                )
+            reduce_z(1)
 
         offset = const.tile([P, HALVES], F32)
         nc.vector.scalar_tensor_tensor(
             out=offset[:], in0=z_total[:], scalar=1.0 / COUNT, in1=neg_shift[:],
             op0=ALU.mult, op1=ALU.add,
         )
+        offset_sq = const.tile([P, HALVES], F32)
+        nc.vector.tensor_mul(out=offset_sq[:], in0=offset[:], in1=offset[:])
+        rest = const.tile([P, HALVES], F32)
+        nc.vector.tensor_sub(out=rest[:], in0=square_part[:], in1=offset_sq[:])
         neg_mean_gain = const.tile([P, HALVES], F32)
         nc.vector.scalar_tensor_tensor(
             out=neg_mean_gain[:], in0=z_total[:], scalar=-1.0 / COUNT, in1=gain_shift[:, 0:HALVES],
             op0=ALU.mult, op1=ALU.mult,
         )
-        offset_sq = const.tile([P, HALVES], F32)
-        nc.vector.tensor_mul(out=offset_sq[:], in0=offset[:], in1=offset[:])
-        rest = const.tile([P, HALVES], F32)
-        nc.vector.tensor_sub(out=rest[:], in0=square_part[:], in1=offset_sq[:])
         inv_std = [const.tile([P, 1], F32, name="inv_std%d" % h) for h in range(HALVES)]
         scale = [const.tile([P, 1], F32, name="scale%d" % h) for h in range(HALVES)]
         bias = [const.tile([P, 1], F32, name="bias%d" % h) for h in range(HALVES)]
@@ -215,13 +226,69 @@ def tile_yuyipointupdate_pb_t_kernel(tc, h1, W2_words, W2_scales, g2, b2, out):
         with ExitStack() as sweep2:
             work = sweep2.enter_context(tc.tile_pool(name="work", bufs=3))
             result_pool = sweep2.enter_context(tc.tile_pool(name="result", bufs=8))
+            rows_pool = sweep2.enter_context(tc.tile_pool(name="rows", bufs=2))
             psum_t = sweep2.enter_context(tc.psum_pool(name="psum_t", bufs=4))
+            rows = work.tile([P, 2, CH_OUT], F32, name="rows")
             z_tiles = {}
             y_tiles = {}
             turned_tiles = {}
             small_tiles = {}
 
+            def by_rows(b):
+                return 0 <= b < GRAPHS - 3 and b % 3 == 2
+
+            def spread_scale_and_bias():
+                turned = psum_t.tile([P, 2, CH_OUT], F32, name="turned")
+                for i, columns in enumerate((scale, bias)):
+                    for h in range(HALVES):
+                        nc.tensor.transpose(
+                            out=turned[:, i, P * h : P * (h + 1)],
+                            in_=columns[h][:].to_broadcast([P, P]),
+                            identity=ident[:],
+                        )
+                nc.scalar.copy(out=rows[:], in_=turned[:])
+
+            def multiply_by_rows(b):
+                for pair in range(NODE_STEP // 2):
+                    z = psum_z.tile([P, 2, CH_OUT], F32, name="z")
+                    for i in range(2):
+                        nodes = slice(P * (2 * pair + i), P * (2 * pair + i + 1))
+                        nc.tensor.matmul_mx(
+                            out=z[:, i, :],
+                            lhsT=h_codes[:, b, nodes].bitcast(FP8X4),
+                            lhsT_scale=h_scales[:, b, nodes],
+                            rhs=w_words[:].bitcast(FP4X4),
+                            rhs_scale=w_scales[:],
+                            start=True,
+                            stop=True,
+                        )
+                    z_tiles[b, pair] = z
+
+            def scale_and_shift_by_rows(b, pair):
+                if pair == 0:
+                    y_tiles[b] = rows_pool.tile([P, NODE_STEP, CH_OUT], F32, name="y_rows")
+                part = y_tiles[b][:, 2 * pair : 2 * pair + 2, :]
+                nc.vector.tensor_mul(
+                    out=part, in0=z_tiles[b, pair][:],
+                    in1=rows[:, 0:1, :].to_broadcast([P, 2, CH_OUT]),
+                )
+                nc.gpsimd.tensor_add(
+                    out=part, in0=part, in1=rows[:, 1:2, :].to_broadcast([P, 2, CH_OUT])
+                )
+
+            def leaky_relu_by_rows(b):
+                result = rows_pool.tile([P, NODE_STEP, CH_OUT], F32, name="result_rows")
+                y_flat = y_tiles[b][:].rearrange("p k o -> p (k o)")
+                nc.vector.scalar_tensor_tensor(
+                    out=result[:].rearrange("p k o -> p (k o)"), in0=y_flat, scalar=NEG_SLOPE,
+                    in1=y_flat, op0=ALU.mult, op1=ALU.max,
+                )
+                nc.sync.dma_start(out=out[b].rearrange("(k q) o -> q k o", q=P), in_=result[:])
+
             def multiply_again(b):
+                if by_rows(b):
+                    multiply_by_rows(b)
+                    return
                 for h in range(HALVES):
                     z = psum_z.tile([P, NODES], F32, name="z")
                     multiply(z[:], b, h, all_nodes, True, True)
@@ -271,15 +338,27 @@ def tile_yuyipointupdate_pb_t_kernel(tc, h1, W2_words, W2_scales, g2, b2, out):
             multiply_again(0)
             multiply_again(1)
             for step in range(GRAPHS + 2):
-                if 0 <= step - 1 < GRAPHS:
+                if 0 <= step - 1 < GRAPHS and not by_rows(step - 1):
                     turn(step - 1)
-                if step < GRAPHS:
+                b = step - 2
+                if by_rows(step):
+                    scale_and_shift_by_rows(step, 1)
+                    normalise(step + 1, 0, "scalar")
+                elif by_rows(step - 1):
+                    normalise(step, 1, "scalar")
+                elif step < GRAPHS:
                     normalise(step, 0, "scalar")
-                    normalise(step, 1, "vector")
+                    normalise(step, 1, "vector" if step < 2 or step > GRAPHS - 3 else "scalar")
+                if step == 0:
+                    spread_scale_and_bias()
+                if by_rows(b):
+                    leaky_relu_by_rows(b)
+                if by_rows(step + 1):
+                    scale_and_shift_by_rows(step + 1, 0)
                 if step + 2 < GRAPHS:
                     multiply_again(step + 2)
-                if 0 <= step - 2:
+                if 0 <= b and not by_rows(b):
                     for pair in range(NODE_STEP // 2):
-                        shrink(step - 2, pair)
+                        shrink(b, pair)
                     for pair in range(NODE_STEP // 2):
-                        leaky_relu_and_store(step - 2, pair)
+                        leaky_relu_and_store(b, pair)

@@ -343,7 +343,6 @@ def tile_yuyipointupdate_pb_t_kernel(tc, h1, W2_words, W2_scales, g2, b2, out):
                 b = step - 2
                 if by_rows(step):
                     scale_and_shift_by_rows(step, 1)
-                    normalise(step + 1, 0, "scalar")
                 elif by_rows(step - 1):
                     normalise(step, 1, "scalar")
                 elif step < GRAPHS:
@@ -362,3 +361,5 @@ def tile_yuyipointupdate_pb_t_kernel(tc, h1, W2_words, W2_scales, g2, b2, out):
                         shrink(b, pair)
                     for pair in range(NODE_STEP // 2):
                         leaky_relu_and_store(b, pair)
+                if by_rows(step):
+                    normalise(step + 1, 0, "scalar")

@@ -140,14 +140,14 @@ def tile_yuyipointupdate_pb_t_kernel(tc, h1, W2_words, W2_scales, g2, b2, out):
 
             def statistics(b):
                 last = b == GRAPHS - 1
-                if last:
-                    for h in range(HALVES):
-                        add_to_sums(b, h)
                 for h in range(HALVES):
                     z = psum_z.tile([P, NODES], F32, name="z")
                     multiply(z[:], b, h, all_nodes, True, True)
                     if not last:
                         add_to_sums(b, h)
+                    elif h == 0:
+                        add_to_sums(b, 0)
+                        add_to_sums(b, 1)
                     squares = junk_pool.tile([P, NODES], F32, name="squares")
                     if b == 0:
                         nc.scalar.mul(out=neg_shift[:, h : h + 1], in_=z[:, 0:1], mul=-1.0)
@@ -164,9 +164,12 @@ def tile_yuyipointupdate_pb_t_kernel(tc, h1, W2_words, W2_scales, g2, b2, out):
             for b in range(GRAPHS):
                 if b + SCALAR_AHEAD < GRAPHS and on_scalar(b + SCALAR_AHEAD):
                     regroup(b + SCALAR_AHEAD)
-                if 1 <= b + 1 < GRAPHS and not on_scalar(b + 1):
+                last_but_one = b == GRAPHS - 2
+                if b + 1 < GRAPHS and not on_scalar(b + 1) and not last_but_one:
                     regroup(b + 1)
                 quantise(b)
+                if last_but_one:
+                    regroup(b + 1)
                 statistics(b)
                 if b == GRAPHS - 3:
                     gb_turned = psum_sum.tile([P, P], BF16)
@@ -225,6 +228,7 @@ def tile_yuyipointupdate_pb_t_kernel(tc, h1, W2_words, W2_scales, g2, b2, out):
 
         with ExitStack() as sweep2:
             work = sweep2.enter_context(tc.tile_pool(name="work", bufs=3))
+            small_pool = sweep2.enter_context(tc.tile_pool(name="small", bufs=6))
             result_pool = sweep2.enter_context(tc.tile_pool(name="result", bufs=8))
             rows_pool = sweep2.enter_context(tc.tile_pool(name="rows", bufs=2))
             psum_t = sweep2.enter_context(tc.psum_pool(name="psum_t", bufs=4))
@@ -323,7 +327,7 @@ def tile_yuyipointupdate_pb_t_kernel(tc, h1, W2_words, W2_scales, g2, b2, out):
                     turned_tiles[b, pair] = turned
 
             def shrink(b, pair):
-                small = work.tile([P, 2, CH_OUT], F32, name="small")
+                small = small_pool.tile([P, 2, CH_OUT], F32, name="small")
                 nc.scalar.mul(out=small[:], in_=turned_tiles[b, pair][:], mul=NEG_SLOPE)
                 small_tiles[b, pair] = small
 
@@ -347,13 +351,13 @@ def tile_yuyipointupdate_pb_t_kernel(tc, h1, W2_words, W2_scales, g2, b2, out):
                     normalise(step, 1, "scalar")
                 elif step < GRAPHS:
                     normalise(step, 0, "scalar")
-                    normalise(step, 1, "vector" if step < 2 or step > GRAPHS - 3 else "scalar")
+                    normalise(step, 1, "vector" if step < 2 or step == GRAPHS - 1 else "scalar")
                 if step == 0:
                     spread_scale_and_bias()
-                if by_rows(b):
-                    leaky_relu_by_rows(b)
                 if by_rows(step + 1):
                     scale_and_shift_by_rows(step + 1, 0)
+                if by_rows(b):
+                    leaky_relu_by_rows(b)
                 if step + 2 < GRAPHS:
                     multiply_again(step + 2)
                 if 0 <= b and not by_rows(b):
@@ -362,4 +366,4 @@ def tile_yuyipointupdate_pb_t_kernel(tc, h1, W2_words, W2_scales, g2, b2, out):
                     for pair in range(NODE_STEP // 2):
                         leaky_relu_and_store(b, pair)
                 if by_rows(step):
-                    normalise(step + 1, 0, "scalar")
+                    normalise(step + 1, 0, "vector" if step == 2 else "scalar")

@@ -75,8 +75,12 @@ def tile_yuyipointupdate_pb_t_kernel(tc, h1, W2_words, W2_scales, g2, b2, out):
         neg_shift = const.tile([P, HALVES], F32)
         square_sums = const.tile([P, HALVES, GRAPHS - 1], F32)
         square_last = const.tile([P, HALVES], F32)
-        z_total = const.tile([P, HALVES], F32)
         square_part = const.tile([P, HALVES], F32)
+        offset = const.tile([P, HALVES], F32)
+        neg_rest = const.tile([P, HALVES], F32)
+        neg_mean_gain = const.tile([P, HALVES], F32)
+        junk_sums = const.tile([P, P], F32)
+        junk_squares = const.tile([P, GRAPHS - 1], F32)
 
         with ExitStack() as sweep1:
             raw_pool = sweep1.enter_context(tc.tile_pool(name="raw", bufs=GRAPHS))
@@ -143,11 +147,7 @@ def tile_yuyipointupdate_pb_t_kernel(tc, h1, W2_words, W2_scales, g2, b2, out):
                 for h in range(HALVES):
                     z = psum_z.tile([P, NODES], F32, name="z")
                     multiply(z[:], b, h, all_nodes, True, True)
-                    if not last:
-                        add_to_sums(b, h)
-                    elif h == 0:
-                        add_to_sums(b, 0)
-                        add_to_sums(b, 1)
+                    add_to_sums(b, h)
                     squares = junk_pool.tile([P, NODES], F32, name="squares")
                     if b == 0:
                         nc.scalar.mul(out=neg_shift[:, h : h + 1], in_=z[:, 0:1], mul=-1.0)
@@ -177,41 +177,38 @@ def tile_yuyipointupdate_pb_t_kernel(tc, h1, W2_words, W2_scales, g2, b2, out):
                     nc.scalar.copy(out=gain_shift[:], in_=gb_turned[:, 0 : 2 * HALVES])
 
             def reduce_z(h):
-                nc.vector.tensor_reduce(
-                    out=z_total[:, h : h + 1], in_=z_sums[h][:], axis=AXIS.X, op=ALU.add
+                nc.vector.tensor_scalar(
+                    out=junk_sums[:], in0=z_sums[h][:], scalar1=1.0 / COUNT,
+                    scalar2=neg_shift[:, h : h + 1], op0=ALU.mult, op1=ALU.add,
+                    accum_out=offset[:, h : h + 1],
                 )
 
             reduce_z(0)
-            nc.vector.tensor_reduce(
-                out=square_part[:], in_=square_sums[:], axis=AXIS.X, op=ALU.add
-            )
-            nc.vector.tensor_scalar(
-                out=square_part[:], in0=square_part[:], scalar1=1.0 / COUNT, scalar2=EPS_BN,
-                op0=ALU.mult, op1=ALU.add,
-            )
+            for h in range(HALVES):
+                nc.vector.tensor_scalar(
+                    out=junk_squares[:], in0=square_sums[:, h, :], scalar1=1.0 / COUNT,
+                    scalar2=EPS_BN, op0=ALU.mult, op1=ALU.add, accum_out=square_part[:, h : h + 1],
+                )
             reduce_z(1)
 
-        offset = const.tile([P, HALVES], F32)
-        nc.vector.scalar_tensor_tensor(
-            out=offset[:], in0=z_total[:], scalar=1.0 / COUNT, in1=neg_shift[:],
-            op0=ALU.mult, op1=ALU.add,
-        )
-        offset_sq = const.tile([P, HALVES], F32)
-        nc.vector.tensor_mul(out=offset_sq[:], in0=offset[:], in1=offset[:])
-        rest = const.tile([P, HALVES], F32)
-        nc.vector.tensor_sub(out=rest[:], in0=square_part[:], in1=offset_sq[:])
-        neg_mean_gain = const.tile([P, HALVES], F32)
-        nc.vector.scalar_tensor_tensor(
-            out=neg_mean_gain[:], in0=z_total[:], scalar=-1.0 / COUNT, in1=gain_shift[:, 0:HALVES],
-            op0=ALU.mult, op1=ALU.mult,
-        )
+        for h in (1, 0):
+            nc.vector.scalar_tensor_tensor(
+                out=neg_rest[:, h : h + 1], in0=offset[:, h : h + 1], scalar=offset[:, h : h + 1],
+                in1=square_part[:, h : h + 1], op0=ALU.mult, op1=ALU.subtract,
+            )
+        for h in range(HALVES):
+            nc.vector.scalar_tensor_tensor(
+                out=neg_mean_gain[:, h : h + 1], in0=neg_shift[:, h : h + 1],
+                scalar=offset[:, h : h + 1], in1=gain_shift[:, h : h + 1],
+                op0=ALU.subtract, op1=ALU.mult,
+            )
         inv_std = [const.tile([P, 1], F32, name="inv_std%d" % h) for h in range(HALVES)]
         scale = [const.tile([P, 1], F32, name="scale%d" % h) for h in range(HALVES)]
         bias = [const.tile([P, 1], F32, name="bias%d" % h) for h in range(HALVES)]
         for h in (1, 0):
             nc.scalar.activation(
                 out=inv_std[h][:], in_=square_last[:, h : h + 1],
-                func=ACT.Abs_reciprocal_sqrt, scale=1.0 / COUNT, bias=rest[:, h : h + 1],
+                func=ACT.Abs_reciprocal_sqrt, scale=-1.0 / COUNT, bias=neg_rest[:, h : h + 1],
             )
         nc.scalar.activation(
             out=scale[0][:], in_=inv_std[0][:], func=ACT.Copy, scale=gain_shift[:, 0:1]

@@ -249,8 +249,8 @@ def tile_yuyipointupdate_pb_t_kernel(tc, h1, W2_words, W2_scales, g2, b2, out):
                         )
                 nc.scalar.copy(out=rows[:], in_=turned[:])
 
-            def multiply_by_rows(b):
-                for pair in range(NODE_STEP // 2):
+            def multiply_by_rows(b, pairs):
+                for pair in pairs:
                     z = psum_z.tile([P, 2, CH_OUT], F32, name="z")
                     for i in range(2):
                         nodes = slice(P * (2 * pair + i), P * (2 * pair + i + 1))
@@ -288,7 +288,7 @@ def tile_yuyipointupdate_pb_t_kernel(tc, h1, W2_words, W2_scales, g2, b2, out):
 
             def multiply_again(b):
                 if by_rows(b):
-                    multiply_by_rows(b)
+                    multiply_by_rows(b, (0,))
                     return
                 for h in range(HALVES):
                     z = psum_z.tile([P, NODES], F32, name="z")
@@ -355,6 +355,8 @@ def tile_yuyipointupdate_pb_t_kernel(tc, h1, W2_words, W2_scales, g2, b2, out):
                     scale_and_shift_by_rows(step + 1, 0)
                 if by_rows(b):
                     leaky_relu_by_rows(b)
+                if by_rows(step + 1):
+                    multiply_by_rows(step + 1, (1,))
                 if step + 2 < GRAPHS:
                     multiply_again(step + 2)
                 if 0 <= b and not by_rows(b):

@@ -88,6 +88,7 @@ def tile_yuyipointupdate_pb_t_kernel(tc, h1, W2_words, W2_scales, g2, b2, out):
             junk_pool = sweep1.enter_context(tc.tile_pool(name="junk", bufs=2))
             psum_sum = sweep1.enter_context(tc.psum_pool(name="psum_sum", bufs=1))
             raw_tiles = {}
+            halves = {}
             grouped_tiles = {}
 
             def load_graph(b):
@@ -119,11 +120,21 @@ def tile_yuyipointupdate_pb_t_kernel(tc, h1, W2_words, W2_scales, g2, b2, out):
                 grouped = grouped_pool.tile([P, NODES, PACK], BF16, align_bytes=64, name="grouped")
                 dst = grouped[:].rearrange("p (c i) t -> p c t i", i=4)
                 src = raw_tiles[b][:].rearrange("p t (c i) -> p c t i", i=4)
-                if on_scalar(b):
+                if b == 1:
+                    half = NODES // 4 // 2
+                    nc.scalar.copy(out=dst[:, 0:half], in_=src[:, 0:half])
+                    halves[b] = (dst, src)
+                elif on_scalar(b):
                     nc.scalar.copy(out=dst, in_=src)
                 else:
                     nc.vector.tensor_copy(out=dst, in_=src)
                 grouped_tiles[b] = grouped
+
+            def second_half(b):
+                if b in halves:
+                    dst, src = halves[b]
+                    half = NODES // 4 // 2
+                    nc.vector.tensor_copy(out=dst[:, half:], in_=src[:, half:])
 
             def quantise(b):
                 nc.vector.quantize_mx(
@@ -165,6 +176,7 @@ def tile_yuyipointupdate_pb_t_kernel(tc, h1, W2_words, W2_scales, g2, b2, out):
                 if b + SCALAR_AHEAD < GRAPHS and on_scalar(b + SCALAR_AHEAD):
                     regroup(b + SCALAR_AHEAD)
                 last_but_one = b == GRAPHS - 2
+                second_half(b + 1)
                 if b + 1 < GRAPHS and not on_scalar(b + 1) and not last_but_one:
                     regroup(b + 1)
                 quantise(b)
@@ -288,7 +300,7 @@ def tile_yuyipointupdate_pb_t_kernel(tc, h1, W2_words, W2_scales, g2, b2, out):
 
             def multiply_again(b):
                 if by_rows(b):
-                    multiply_by_rows(b, (0,))
+                    multiply_by_rows(b, (0,) if b > 2 else (0, 1))
                     return
                 for h in range(HALVES):
                     z = psum_z.tile([P, NODES], F32, name="z")
@@ -355,7 +367,7 @@ def tile_yuyipointupdate_pb_t_kernel(tc, h1, W2_words, W2_scales, g2, b2, out):
                     scale_and_shift_by_rows(step + 1, 0)
                 if by_rows(b):
                     leaky_relu_by_rows(b)
-                if by_rows(step + 1):
+                if by_rows(step + 1) and step > 1:
                     multiply_by_rows(step + 1, (1,))
                 if step + 2 < GRAPHS:
                     multiply_again(step + 2)

@@ -237,7 +237,7 @@ def tile_yuyipointupdate_pb_t_kernel(tc, h1, W2_words, W2_scales, g2, b2, out):
 
         with ExitStack() as sweep2:
             work = sweep2.enter_context(tc.tile_pool(name="work", bufs=3))
-            small_pool = sweep2.enter_context(tc.tile_pool(name="small", bufs=6))
+            copied_pool = sweep2.enter_context(tc.tile_pool(name="copied", bufs=6))
             result_pool = sweep2.enter_context(tc.tile_pool(name="result", bufs=8))
             rows_pool = sweep2.enter_context(tc.tile_pool(name="rows", bufs=2))
             psum_t = sweep2.enter_context(tc.psum_pool(name="psum_t", bufs=4))
@@ -245,7 +245,7 @@ def tile_yuyipointupdate_pb_t_kernel(tc, h1, W2_words, W2_scales, g2, b2, out):
             z_tiles = {}
             y_tiles = {}
             turned_tiles = {}
-            small_tiles = {}
+            copied_tiles = {}
 
             def by_rows(b):
                 return 0 <= b < GRAPHS - 3 and b % 3 == 2
@@ -335,16 +335,17 @@ def tile_yuyipointupdate_pb_t_kernel(tc, h1, W2_words, W2_scales, g2, b2, out):
                             )
                     turned_tiles[b, pair] = turned
 
-            def shrink(b, pair):
-                small = small_pool.tile([P, 2, CH_OUT], F32, name="small")
-                nc.scalar.mul(out=small[:], in_=turned_tiles[b, pair][:], mul=NEG_SLOPE)
-                small_tiles[b, pair] = small
+            def copy_out(b, pair):
+                copied = copied_pool.tile([P, 2, CH_OUT], F32, name="copied")
+                nc.scalar.copy(out=copied[:], in_=turned_tiles[b, pair][:])
+                copied_tiles[b, pair] = copied
 
             def leaky_relu_and_store(b, pair):
                 rows = out[b].rearrange("(q j) o -> q j o", j=NODE_STEP)
                 result = result_pool.tile([P, 2, CH_OUT], F32, name="result")
-                nc.vector.tensor_max(
-                    out=result[:], in0=turned_tiles[b, pair][:], in1=small_tiles[b, pair][:]
+                nc.vector.scalar_tensor_tensor(
+                    out=result[:], in0=turned_tiles[b, pair][:], scalar=NEG_SLOPE,
+                    in1=copied_tiles[b, pair][:], op0=ALU.mult, op1=ALU.max,
                 )
                 nc.sync.dma_start(out=rows[:, 2 * pair : 2 * pair + 2, :], in_=result[:])
 
@@ -373,7 +374,7 @@ def tile_yuyipointupdate_pb_t_kernel(tc, h1, W2_words, W2_scales, g2, b2, out):
                     multiply_again(step + 2)
                 if 0 <= b and not by_rows(b):
                     for pair in range(NODE_STEP // 2):
-                        shrink(b, pair)
+                        copy_out(b, pair)
                     for pair in range(NODE_STEP // 2):
                         leaky_relu_and_store(b, pair)
                 if by_rows(step):

from contextlib import ExitStack

import concourse.mybir as mybir
from concourse.masks import make_identity

F32 = mybir.dt.float32
BF16 = mybir.dt.bfloat16
I32 = mybir.dt.int32
U8 = mybir.dt.uint8
U32 = mybir.dt.uint32
FP8X4 = mybir.dt.float8_e4m3fn_x4
FP4X4 = mybir.dt.float4_e2m1fn_x4
ALU = mybir.AluOpType
ACT = mybir.ActivationFunctionType
AXIS = mybir.AxisListType

P = 128
PACK = 4
GRAPHS = 24
NODES = 512
CH_IN = P * PACK
CH_OUT = 256
HALVES = CH_OUT // P
COUNT = GRAPHS * NODES
EPS_BN = 1e-5
NEG_SLOPE = 0.01
NODE_STEP = NODES // P

FLOPS = 2 * GRAPHS * NODES * CH_IN * CH_OUT


SCALAR_EVERY = 6
SCALAR_AHEAD = 4


def tile_yuyipointupdate_pb_t_kernel(tc, h1, W2_words, W2_scales, g2, b2, out):
    nc = tc.nc
    with ExitStack() as pools:
        pools.enter_context(tc.manual_schedule())
        const = pools.enter_context(tc.tile_pool(name="const", bufs=1))
        psum_z = pools.enter_context(tc.psum_pool(name="psum_z", bufs=4))

        one = const.tile([P, 1], F32)
        nc.vector.memset(one[:], 1.0)
        one_root = const.tile([P, 1], F32)
        nc.scalar.activation(out=one_root[:], in_=one[:], func=ACT.Abs_reciprocal_sqrt)

        ident_bf16 = const.tile([P, P], BF16)
        make_identity(nc, ident_bf16[:])
        ident = const.tile([P, P], F32)
        make_identity(nc, ident[:])

        h_codes = const.tile([P, GRAPHS, NODES], U32, align_bytes=64)
        h_scales = const.tile([P, GRAPHS, NODES], U8, align_bytes=64)
        w_words = const.tile([P, 2 * CH_OUT], U8, align_bytes=64)
        w_scales = const.tile([P, CH_OUT], U8, align_bytes=64)
        gb_rows = const.tile([P, P], BF16)
        gain_shift = const.tile([P, 2 * HALVES], F32)
        nc.vector.memset(w_scales[:].bitcast(I32), 0)
        nc.vector.memset(gb_rows[:], 0.0)

        def multiply(acc, b, h, nodes, start, stop):
            nc.tensor.matmul_mx(
                out=acc,
                lhsT=w_words[:, 2 * P * h : 2 * P * (h + 1)].bitcast(FP4X4),
                lhsT_scale=w_scales[:, P * h : P * (h + 1)],
                rhs=h_codes[:, b, nodes].bitcast(FP8X4),
                rhs_scale=h_scales[:, b, nodes],
                start=start,
                stop=stop,
            )

        all_nodes = slice(0, NODES)

        neg_shift = const.tile([P, HALVES], F32)
        square_sums = const.tile([P, HALVES, GRAPHS - 1], F32)
        square_last = const.tile([P, HALVES], F32)
        square_part = const.tile([P, HALVES], F32)
        offset = const.tile([P, HALVES], F32)
        neg_rest = const.tile([P, HALVES], F32)
        neg_mean_gain = const.tile([P, HALVES], F32)
        junk_sums = const.tile([P, P], F32)
        junk_squares = const.tile([P, GRAPHS - 1], F32)

        with ExitStack() as sweep1:
            raw_pool = sweep1.enter_context(tc.tile_pool(name="raw", bufs=GRAPHS))
            grouped_pool = sweep1.enter_context(tc.tile_pool(name="grouped", bufs=4))
            junk_pool = sweep1.enter_context(tc.tile_pool(name="junk", bufs=2))
            psum_sum = sweep1.enter_context(tc.psum_pool(name="psum_sum", bufs=1))
            raw_tiles = {}
            halves = {}
            grouped_tiles = {}

            def load_graph(b):
                raw = raw_pool.tile([P, PACK, NODES], BF16, name="raw")
                nc.sync.dma_start(out=raw[:], in_=h1[b].rearrange("(p t) n -> p t n", t=PACK))
                raw_tiles[b] = raw

            for b in range(3):
                load_graph(b)
            nc.sync.dma_start(out=w_words[:].bitcast(I32), in_=W2_words[0].bitcast(I32))
            for quadrant in range(4):
                nc.sync.dma_start(
                    out=w_scales[32 * quadrant : 32 * quadrant + 4, :].bitcast(I32),
                    in_=W2_scales[0, 4 * quadrant : 4 * quadrant + 4, :].bitcast(I32),
                )
            for b in (3, 7, 4, 5, 6):
                load_graph(b)
            for b in range(8, GRAPHS):
                load_graph(b)
            nc.sync.dma_start(out=gb_rows[0:HALVES, :], in_=g2.rearrange("(h o) -> h o", h=HALVES))
            nc.sync.dma_start(
                out=gb_rows[HALVES : 2 * HALVES, :], in_=b2.rearrange("(h o) -> h o", h=HALVES)
            )

            def on_scalar(b):
                return b % SCALAR_EVERY == 1

            def regroup(b):
                grouped = grouped_pool.tile([P, NODES, PACK], BF16, align_bytes=64, name="grouped")
                dst = grouped[:].rearrange("p (c i) t -> p c t i", i=4)
                src = raw_tiles[b][:].rearrange("p t (c i) -> p c t i", i=4)
                if b == 1:
                    half = NODES // 4 // 2
                    nc.scalar.copy(out=dst[:, 0:half], in_=src[:, 0:half])
                    halves[b] = (dst, src)
                elif on_scalar(b):
                    nc.scalar.copy(out=dst, in_=src)
                else:
                    nc.vector.tensor_copy(out=dst, in_=src)
                grouped_tiles[b] = grouped

            def second_half(b):
                if b in halves:
                    dst, src = halves[b]
                    half = NODES // 4 // 2
                    nc.vector.tensor_copy(out=dst[:, half:], in_=src[:, half:])

            def quantise(b):
                nc.vector.quantize_mx(
                    out=h_codes[:, b, :].bitcast(FP8X4),
                    scales=h_scales[:, b, :],
                    in_=grouped_tiles[b][:].rearrange("p n t -> p (n t)"),
                )

            z_sums = [psum_sum.tile([P, P], F32, name="z_sum%d" % h) for h in range(HALVES)]

            def add_to_sums(b, h):
                for block in range(NODE_STEP):
                    multiply(
                        z_sums[h][:], b, h, slice(P * block, P * (block + 1)),
                        b == 0 and block == 0,
                        b == GRAPHS - 1 and block == NODE_STEP - 1,
                    )

            def statistics(b):
                last = b == GRAPHS - 1
                for h in range(HALVES):
                    z = psum_z.tile([P, NODES], F32, name="z")
                    multiply(z[:], b, h, all_nodes, True, True)
                    add_to_sums(b, h)
                    squares = junk_pool.tile([P, NODES], F32, name="squares")
                    if b == 0:
                        nc.scalar.mul(out=neg_shift[:, h : h + 1], in_=z[:, 0:1], mul=-1.0)
                    nc.scalar.activation(
                        out=squares[:], in_=z[:], func=ACT.Square,
                        bias=neg_shift[:, h : h + 1],
                        accum_out=(
                            square_sums[:, h, b : b + 1] if b < GRAPHS - 1 else square_last[:, h : h + 1]
                        ),
                    )

            regroup(0)
            regroup(1)
            for b in range(GRAPHS):
                if b + SCALAR_AHEAD < GRAPHS and on_scalar(b + SCALAR_AHEAD):
                    regroup(b + SCALAR_AHEAD)
                last_but_one = b == GRAPHS - 2
                second_half(b + 1)
                if b + 1 < GRAPHS and not on_scalar(b + 1) and not last_but_one:
                    regroup(b + 1)
                quantise(b)
                if last_but_one:
                    regroup(b + 1)
                statistics(b)
                if b == GRAPHS - 3:
                    gb_turned = psum_sum.tile([P, P], BF16)
                    nc.tensor.transpose(out=gb_turned[:], in_=gb_rows[:], identity=ident_bf16[:])
                    nc.scalar.copy(out=gain_shift[:], in_=gb_turned[:, 0 : 2 * HALVES])

            def reduce_z(h):
                nc.vector.tensor_scalar(
                    out=junk_sums[:], in0=z_sums[h][:], scalar1=1.0 / COUNT,
                    scalar2=neg_shift[:, h : h + 1], op0=ALU.mult, op1=ALU.add,
                    accum_out=offset[:, h : h + 1],
                )

            reduce_z(0)
            for h in range(HALVES):
                nc.vector.tensor_scalar(
                    out=junk_squares[:], in0=square_sums[:, h, :], scalar1=1.0 / COUNT,
                    scalar2=EPS_BN, op0=ALU.mult, op1=ALU.add, accum_out=square_part[:, h : h + 1],
                )
            reduce_z(1)

        for h in (1, 0):
            nc.vector.scalar_tensor_tensor(
                out=neg_rest[:, h : h + 1], in0=offset[:, h : h + 1], scalar=offset[:, h : h + 1],
                in1=square_part[:, h : h + 1], op0=ALU.mult, op1=ALU.subtract,
            )
        for h in range(HALVES):
            nc.vector.scalar_tensor_tensor(
                out=neg_mean_gain[:, h : h + 1], in0=neg_shift[:, h : h + 1],
                scalar=offset[:, h : h + 1], in1=gain_shift[:, h : h + 1],
                op0=ALU.subtract, op1=ALU.mult,
            )
        inv_std = [const.tile([P, 1], F32, name="inv_std%d" % h) for h in range(HALVES)]
        scale = [const.tile([P, 1], F32, name="scale%d" % h) for h in range(HALVES)]
        bias = [const.tile([P, 1], F32, name="bias%d" % h) for h in range(HALVES)]
        for h in (1, 0):
            nc.scalar.activation(
                out=inv_std[h][:], in_=square_last[:, h : h + 1],
                func=ACT.Abs_reciprocal_sqrt, scale=-1.0 / COUNT, bias=neg_rest[:, h : h + 1],
            )
        nc.scalar.activation(
            out=scale[0][:], in_=inv_std[0][:], func=ACT.Copy, scale=gain_shift[:, 0:1]
        )
        nc.scalar.activation(
            out=bias[0][:], in_=inv_std[0][:], func=ACT.Identity,
            scale=neg_mean_gain[:, 0:1], bias=gain_shift[:, HALVES : HALVES + 1],
        )
        nc.vector.tensor_mul(out=scale[1][:], in0=gain_shift[:, 1:2], in1=inv_std[1][:])
        nc.vector.scalar_tensor_tensor(
            out=bias[1][:], in0=inv_std[1][:], scalar=neg_mean_gain[:, 1:2],
            in1=gain_shift[:, HALVES + 1 : HALVES + 2], op0=ALU.mult, op1=ALU.add,
        )

        with ExitStack() as sweep2:
            work = sweep2.enter_context(tc.tile_pool(name="work", bufs=3))
            copied_pool = sweep2.enter_context(tc.tile_pool(name="copied", bufs=6))
            result_pool = sweep2.enter_context(tc.tile_pool(name="result", bufs=8))
            rows_pool = sweep2.enter_context(tc.tile_pool(name="rows", bufs=2))
            psum_t = sweep2.enter_context(tc.psum_pool(name="psum_t", bufs=4))
            rows = work.tile([P, 2, CH_OUT], F32, name="rows")
            z_tiles = {}
            y_tiles = {}
            turned_tiles = {}
            copied_tiles = {}

            def by_rows(b):
                return 0 <= b < GRAPHS - 3 and b % 3 == 2

            def spread_scale_and_bias():
                turned = psum_t.tile([P, 2, CH_OUT], F32, name="turned")
                for i, columns in enumerate((scale, bias)):
                    for h in range(HALVES):
                        nc.tensor.transpose(
                            out=turned[:, i, P * h : P * (h + 1)],
                            in_=columns[h][:].to_broadcast([P, P]),
                            identity=ident[:],
                        )
                nc.scalar.copy(out=rows[:], in_=turned[:])

            def multiply_by_rows(b, pairs):
                for pair in pairs:
                    z = psum_z.tile([P, 2, CH_OUT], F32, name="z")
                    for i in range(2):
                        nodes = slice(P * (2 * pair + i), P * (2 * pair + i + 1))
                        nc.tensor.matmul_mx(
                            out=z[:, i, :],
                            lhsT=h_codes[:, b, nodes].bitcast(FP8X4),
                            lhsT_scale=h_scales[:, b, nodes],
                            rhs=w_words[:].bitcast(FP4X4),
                            rhs_scale=w_scales[:],
                            start=True,
                            stop=True,
                        )
                    z_tiles[b, pair] = z

            def scale_and_shift_by_rows(b, pair):
                if pair == 0:
                    y_tiles[b] = rows_pool.tile([P, NODE_STEP, CH_OUT], F32, name="y_rows")
                part = y_tiles[b][:, 2 * pair : 2 * pair + 2, :]
                nc.vector.tensor_mul(
                    out=part, in0=z_tiles[b, pair][:],
                    in1=rows[:, 0:1, :].to_broadcast([P, 2, CH_OUT]),
                )
                nc.gpsimd.tensor_add(
                    out=part, in0=part, in1=rows[:, 1:2, :].to_broadcast([P, 2, CH_OUT])
                )

            def leaky_relu_by_rows(b):
                result = rows_pool.tile([P, NODE_STEP, CH_OUT], F32, name="result_rows")
                y_flat = y_tiles[b][:].rearrange("p k o -> p (k o)")
                nc.vector.scalar_tensor_tensor(
                    out=result[:].rearrange("p k o -> p (k o)"), in0=y_flat, scalar=NEG_SLOPE,
                    in1=y_flat, op0=ALU.mult, op1=ALU.max,
                )
                nc.sync.dma_start(out=out[b].rearrange("(k q) o -> q k o", q=P), in_=result[:])

            def multiply_again(b):
                if by_rows(b):
                    multiply_by_rows(b, (0,) if b > 2 else (0, 1))
                    return
                for h in range(HALVES):
                    z = psum_z.tile([P, NODES], F32, name="z")
                    multiply(z[:], b, h, all_nodes, True, True)
                    z_tiles[b, h] = z
                y_tiles[b] = work.tile([P, HALVES, NODES], F32, name="y")

            def normalise(b, h, engine):
                y = y_tiles[b][:, h, :].rearrange("p (j q) -> p j q", j=NODE_STEP)
                z = z_tiles[b, h][:].rearrange("p (q j) -> p j q", j=NODE_STEP)
                if engine == "scalar":
                    nc.scalar.activation(
                        out=y, in_=z, func=ACT.Identity,
                        scale=scale[h][:], bias=bias[h][:],
                    )
                else:
                    nc.vector.tensor_scalar(
                        out=y, in0=z, scalar1=scale[h][:], scalar2=bias[h][:],
                        op0=ALU.mult, op1=ALU.add,
                    )

            def turn(b):
                for pair in range(NODE_STEP // 2):
                    turned = psum_t.tile([P, 2, CH_OUT], F32, name="turned")
                    for i in range(2):
                        j = 2 * pair + i
                        for h in range(HALVES):
                            nc.tensor.transpose(
                                out=turned[:, i, P * h : P * (h + 1)],
                                in_=y_tiles[b][:, h, P * j : P * (j + 1)],
                                identity=ident[:],
                            )
                    turned_tiles[b, pair] = turned

            def copy_out(b, pair):
                copied = copied_pool.tile([P, 2, CH_OUT], F32, name="copied")
                nc.scalar.copy(out=copied[:], in_=turned_tiles[b, pair][:])
                copied_tiles[b, pair] = copied

            def leaky_relu_and_store(b, pair):
                rows = out[b].rearrange("(q j) o -> q j o", j=NODE_STEP)
                result = result_pool.tile([P, 2, CH_OUT], F32, name="result")
                nc.vector.scalar_tensor_tensor(
                    out=result[:], in0=turned_tiles[b, pair][:], scalar=NEG_SLOPE,
                    in1=copied_tiles[b, pair][:], op0=ALU.mult, op1=ALU.max,
                )
                nc.sync.dma_start(out=rows[:, 2 * pair : 2 * pair + 2, :], in_=result[:])

            multiply_again(0)
            multiply_again(1)
            for step in range(GRAPHS + 2):
                if 0 <= step - 1 < GRAPHS and not by_rows(step - 1):
                    turn(step - 1)
                b = step - 2
                if by_rows(step):
                    scale_and_shift_by_rows(step, 1)
                elif by_rows(step - 1):
                    normalise(step, 1, "scalar")
                elif step < GRAPHS:
                    normalise(step, 0, "scalar")
                    normalise(step, 1, "vector" if step < 2 or step == GRAPHS - 1 else "scalar")
                if step == 0:
                    spread_scale_and_bias()
                if by_rows(step + 1):
                    scale_and_shift_by_rows(step + 1, 0)
                if by_rows(b):
                    leaky_relu_by_rows(b)
                if by_rows(step + 1) and step > 1:
                    multiply_by_rows(step + 1, (1,))
                if step + 2 < GRAPHS:
                    multiply_again(step + 2)
                if 0 <= b and not by_rows(b):
                    for pair in range(NODE_STEP // 2):
                        copy_out(b, pair)
                    for pair in range(NODE_STEP // 2):
                        leaky_relu_and_store(b, pair)
                if by_rows(step):
                    normalise(step + 1, 0, "vector" if step == 2 else "scalar")
